import numpy as np
import ml_dtypes


def mxq(x, axis, fmt="e4m3"):
    dtype, down = {"e4m3": (ml_dtypes.float8_e4m3fn, 7), "e5m2": (ml_dtypes.float8_e5m2, 14)}[fmt]
    v = np.moveaxis(np.asarray(x, np.float32).astype(ml_dtypes.bfloat16).astype(np.float64), axis, -1)
    blocks = v.reshape(v.shape[:-1] + (-1, 32))
    amax = np.abs(blocks).max(-1, keepdims=True)
    byte = np.maximum(np.where(amax > 0, np.frexp(amax)[1] - 1 + 127, 0) - down, 1)
    scale = np.exp2(byte - 127.0)
    codes = (blocks / scale).astype(np.float32).astype(dtype).astype(np.float64)
    return np.moveaxis((codes * scale).reshape(v.shape), -1, axis)


WIDE = False


def mx_kscale(k):
    if not WIDE:
        return np.ones(k)
    levels = np.array([10, -10, 5, -5, 0])
    if k % 512:
        return np.exp2(np.random.permutation(np.resize(levels, k // 32))).repeat(32)
    a = np.empty((k // 512, 16))
    for p in range(k // 512):
        a[p, :8] = np.random.permutation(np.resize(levels, 8))
        for g in range(8):
            far = levels[np.abs(levels - a[p, g]) >= 10]
            a[p, g + 8] = far[np.random.randint(len(far))]
    return np.exp2(a.ravel()).repeat(32)


BF16 = ml_dtypes.bfloat16


def bf(x):
    return np.asarray(x, np.float32).astype(BF16)


def f64(x):
    return np.asarray(x).astype(np.float64)


E2M1 = np.array([0.0, 0.5, 1.0, 1.5, 2.0, 3.0, 4.0, 6.0, -0.0, -0.5, -1.0, -1.5, -2.0, -3.0, -4.0, -6.0])


def pack_weight(w, fmt):
    k, n = w.shape
    w = f64(bf(w)).reshape(k // 32, 32, n)
    amax = np.abs(w).max(1)
    if fmt == "e4m3":
        byte = np.frexp(amax)[1] - 1 + 127 - 7
    else:
        mant, ex = np.frexp(amax / 6.0)
        byte = np.where(mant > 0.5, ex, ex - 1) + 127
    byte = np.clip(np.where(amax > 0, byte, 1), 1, 254)
    scaled = (w * np.exp2(127.0 - byte)[:, None, :]).reshape(k, n).astype(np.float32)
    by_word = np.ascontiguousarray(scaled.reshape(k // 512, 128, 4, n).transpose(0, 1, 3, 2))
    if fmt == "e4m3":
        words = by_word.astype(ml_dtypes.float8_e4m3fn).view(np.uint8)
    else:
        c = by_word.astype(ml_dtypes.float4_e2m1fn).view(np.uint8) & 0xF
        words = c[..., 0::2] | (c[..., 1::2] << 4)
    return np.ascontiguousarray(words), np.ascontiguousarray(byte.astype(np.uint8).reshape(k // 512, 16, n))


def unpack_weight(words, scales, fmt):
    g, p, n, _ = words.shape
    if fmt == "e4m3":
        vals = np.ascontiguousarray(words).view(ml_dtypes.float8_e4m3fn).astype(np.float64)
    else:
        nib = np.empty((g, p, n, 4), np.uint8)
        nib[..., 0::2] = words & 0xF
        nib[..., 1::2] = words >> 4
        vals = E2M1[nib]
    vals = vals * np.repeat(np.exp2(scales.astype(np.float64) - 127.0), 8, axis=1)[..., None]
    return vals.transpose(0, 1, 3, 2).reshape(g * 512, n)
def pack4(w):
    words, scales = pack_weight(w, "e2m1")
    return words.reshape(words.shape[0], 128, -1), scales


def unpack4(words, scales):
    return unpack_weight(words.reshape(words.shape[0], 128, -1, 2), scales, "e2m1")


H, L, B, S = 512, 2, 1024, 16


def sigmoid(v):
    return 1.0 / (1.0 + np.exp(-v))


def draw0():
    r = np.random.standard_normal
    s, t, u = mx_kscale(H), mx_kscale(H), mx_kscale(H)
    st = np.concatenate([s, t])
    x = bf(r((B, H)) * s)
    enc_seq = bf(r((S, B, H)) * t)
    attn_W_words, attn_W_scales = pack4((r((H, H)) / np.sqrt(H) / s[None, :] / t[:, None]).T)
    attn_b = bf(r(H) * 0.5 / t)
    h_prev = bf(r((B, H)) * u)
    c_prev = bf(r((B, H)))
    W_ih0_words, W_ih0_scales = pack4((r((4 * H, H + H)) * 0.6 / np.sqrt(H) / st[None, :]).T)
    W_hh0_words, W_hh0_scales = pack4((r((4 * H, H)) * 0.6 / np.sqrt(H) / u[None, :]).T)
    return {
        "x": x,
        "enc_seq": enc_seq,
        "attn_W_words": attn_W_words,
        "attn_W_scales": attn_W_scales,
        "attn_b": attn_b,
        "h_prev": h_prev,
        "c_prev": c_prev,
        "W_ih0_words": W_ih0_words,
        "W_ih0_scales": W_ih0_scales,
        "W_hh0_words": W_hh0_words,
        "W_hh0_scales": W_hh0_scales,
        "b_ih0": bf(r(4 * H) * 0.3),
        "b_hh0": bf(r(4 * H) * 0.3),
    }


def core(x, enc_seq, attn_W_words, attn_W_scales, attn_b, h_prev, c_prev, W_ih0_words, W_ih0_scales, W_hh0_words, W_hh0_scales, b_ih0, b_hh0):
    enc = f64(enc_seq)
    xq = mxq(f64(x), 1, "e4m3")
    attn_lin = (xq @ unpack4(attn_W_words, attn_W_scales)) + f64(attn_b)
    scores = attn_lin[None, :, :] * enc
    e = np.exp(scores - scores.max(0, keepdims=True))
    w = e / e.sum(0, keepdims=True)
    attention = (enc * w).sum(0)
    aq = mxq(attention, 1, "e4m3")
    w_ih = unpack4(W_ih0_words, W_ih0_scales)
    w_x = w_ih[:H]
    w_a = w_ih[H:]
    hq = mxq(f64(h_prev), 1, "e4m3")
    gates = (xq @ w_x) + (aq @ w_a) + f64(b_ih0) + (hq @ unpack4(W_hh0_words, W_hh0_scales)) + f64(b_hh0)
    i, f, g, o = np.split(gates, 4, axis=-1)
    c_new = sigmoid(f) * f64(c_prev) + sigmoid(i) * np.tanh(g)
    h_new = sigmoid(o) * np.tanh(c_new)
    return h_new, c_new


def e4m3fn_bytes(y):
    return np.clip(np.asarray(y, np.float64), -448.0, 448.0).astype(np.float32).astype(ml_dtypes.float8_e4m3fn).view(np.uint8)


def e4m3fn_values(b):
    return np.asarray(b, np.uint8).view(ml_dtypes.float8_e4m3fn).astype(np.float64)


def setup_inputs():
    d = draw0()
    x0 = np.asarray(d['x']).astype(np.float64)
    s = (np.max(np.abs(x0), axis=(0,), keepdims=True) / 448.0).astype(np.float32)
    out = {}
    for k, v in d.items():
        if k == 'x':
            out['x_bytes'] = e4m3fn_bytes(x0 / s.astype(np.float64))
            out['x_scale'] = s
        else:
            out[k] = v
    return out


def reference(x_bytes, x_scale, enc_seq, attn_W_words, attn_W_scales, attn_b, h_prev, c_prev, W_ih0_words, W_ih0_scales, W_hh0_words, W_hh0_scales, b_ih0, b_hh0):
    return core(e4m3fn_values(x_bytes) * x_scale.astype(np.float64), enc_seq, attn_W_words, attn_W_scales, attn_b, h_prev, c_prev, W_ih0_words, W_ih0_scales, W_hh0_words, W_hh0_scales, b_ih0, b_hh0)

@@ -1,0 +1,462 @@
+from contextlib import ExitStack
+
+import concourse.mybir as mybir
+from concourse.masks import make_identity
+
+B, H, S = 1024, 512, 16
+P = 128
+TILES = B // P
+CHUNKS = H // P
+FLOPS = 2 * B * H * (H + 3 * 4 * H)
+
+F32 = mybir.dt.float32
+BF16 = mybir.dt.bfloat16
+I32 = mybir.dt.int32
+U32 = mybir.dt.uint32
+U8 = mybir.dt.uint8
+FP8 = mybir.dt.float8_e4m3fn
+FP8X4 = mybir.dt.float8_e4m3fn_x4
+FP4X4 = mybir.dt.float4_e2m1fn_x4
+ACT = mybir.ActivationFunctionType
+ALU = mybir.AluOpType
+
+GPSIMD_DIFF = 13
+GATE_I, GATE_F, GATE_G, GATE_O = 0, 1, 2, 3
+
+
+def tile_decoderlstm_pa_t_w4_kernel(
+    tc, x_bytes, x_scale, enc_seq, attn_W_words, attn_W_scales, attn_b, h_prev, c_prev,
+    W_ih0_words, W_ih0_scales, W_hh0_words, W_hh0_scales, b_ih0, b_hh0, out_0, out_1,
+):
+    nc = tc.nc
+    with ExitStack() as ctx:
+        sb = ctx.enter_context(tc.tile_pool(name="sb", bufs=1))
+        ps = ctx.enter_context(tc.psum_pool(name="ps", bufs=1))
+        ctx.enter_context(tc.manual_schedule())
+
+        def sbuf(name, shape, dtype):
+            return sb.tile(shape, dtype, name=name, align_bytes=64)
+
+        def bank(name):
+            return ps.tile([P, H], F32, name=name)
+
+        abs_bank, sign_bank, max_bank = bank("abs_bank"), bank("sign_bank"), bank("max_bank")
+        den_bank, num_bank = bank("den_bank"), bank("num_bank")
+        bank_a, bank_b, bank_c = bank("bank_a"), bank("bank_b"), bank("bank_c")
+
+        ident32 = sbuf("ident32", [P, P], F32)
+        ident16 = sbuf("ident16", [P, P], BF16)
+        ones = sbuf("ones", [P, P], F32)
+        bias_rows = sbuf("bias_rows", [P, P], BF16)
+        bias_cols = sbuf("bias_cols", [P, 36], F32)
+        gate_bias = sbuf("gate_bias", [P, 16], F32)
+        half_gate_bias = sbuf("half_gate_bias", [P, 16], F32)
+        xs = sbuf("xs", [P, 4], F32)
+        xb_first = sbuf("xb_first", [P, H], U8)
+        xb_rest = sbuf("xb_rest", [P, TILES - 1, H], U8)
+        h_first = sbuf("h_first", [P, H], BF16)
+        h_rest = sbuf("h_rest", [P, TILES - 1, H], BF16)
+        c_all = sbuf("c_all", [P, TILES, H], BF16)
+        wa_words = sbuf("wa_words", [P, 2 * H], U8)
+        wa_scales = sbuf("wa_scales", [P, H], U8)
+        wih_words = sbuf("wih_words", [P, 2, 8 * H], U8)
+        wih_scales = sbuf("wih_scales", [P, 2, 4 * H], U8)
+        whh_words = sbuf("whh_words", [P, 8 * H], U8)
+        whh_scales = sbuf("whh_scales", [P, 4 * H], U8)
+
+        enc = [sbuf("enc%d" % n, [P, S, H], BF16) for n in range(3)]
+        signed = sbuf("signed", [P, S, H], BF16)
+        level = [sbuf("level%d" % n, [P, S >> (n + 1), H], BF16) for n in range(4)]
+        top = level[3]
+        work = [sbuf("work%d" % n, [P, S, P], F32) for n in range(CHUNKS + 1)]
+        prod = [sbuf("prod%d" % n, [P, S, P], F32) for n in range(3)]
+
+        x_wide = sbuf("x_wide", [P, H], BF16)
+        xh_grouped = sbuf("xh_grouped", [P, 2 * H], BF16)
+        xh_codes = [sbuf("xh_codes%d" % n, [P, 2 * P], U32) for n in range(TILES)]
+        xh_scales = [sbuf("xh_scales%d" % n, [P, 2 * P], U8) for n in range(TILES)]
+        abs_t = sbuf("abs_t", [P, H], F32)
+        sign_t = sbuf("sign_t", [P, H], BF16)
+        log_den = sbuf("log_den", [P, H], F32)
+        inv_den = sbuf("inv_den", [P, H], F32)
+        att_t = sbuf("att_t", [P, H], BF16)
+        att_rows = sbuf("att_rows", [P, H], BF16)
+        att_grouped = sbuf("att_grouped", [P, H], BF16)
+        att_codes = sbuf("att_codes", [P, P], U32)
+        att_scales = sbuf("att_scales", [P, P], U8)
+        gate_t = [sbuf("gate_t%d" % n, [P, H], F32) for n in range(4)]
+        keep_t = sbuf("keep_t", [P, H], F32)
+        write_t = sbuf("write_t", [P, H], F32)
+        tanh_c = sbuf("tanh_c", [P, H], F32)
+        c_out = [sbuf("c_out%d" % n, [P, H], F32) for n in range(2)]
+        h_out = [sbuf("h_out%d" % n, [P, H], F32) for n in range(2)]
+
+        def cols(c):
+            return slice(c * P, (c + 1) * P)
+
+        def rows(i):
+            return slice(i * P, (i + 1) * P)
+
+        def over_s(ap, count=S):
+            return ap.unsqueeze(1).to_broadcast([P, count, P])
+
+        def as_bf16(psum_tile):
+            return psum_tile[:].bitcast(BF16)[:, 0:H]
+
+        def work_of(i, c):
+            return work[c + (i % 2 if c == CHUNKS - 1 else 0)]
+
+        def prod_of(i, c):
+            return prod[(CHUNKS * i + c) % 3]
+
+        def load_scales(plane, scales):
+            for q in range(4):
+                nc.sync.dma_start(out=plane[32 * q : 32 * q + 4].bitcast(I32), in_=scales(slice(4 * q, 4 * q + 4)))
+
+        def load_enc(i):
+            for half in range(2):
+                ss = slice(half * S // 2, (half + 1) * S // 2)
+                nc.sync.dma_start(out=enc[i % 3][:, ss, :], in_=enc_seq[ss, rows(i), :].rearrange("s b j -> b s j"))
+
+        nc.gpsimd.memset(wa_scales[:].bitcast(I32), 0)
+        nc.gpsimd.memset(bias_rows[:], 0.0)
+        make_identity(nc, ident32[:])
+        make_identity(nc, ident16[:])
+        nc.gpsimd.memset(ones[:], 1.0)
+        nc.gpsimd.memset(wih_scales[:].bitcast(I32), 0)
+        nc.gpsimd.memset(whh_scales[:].bitcast(I32), 0)
+
+        nc.sync.dma_start(out=xb_first[:], in_=x_bytes[rows(0), :])
+        nc.sync.dma_start(out=h_first[:], in_=h_prev[rows(0), :])
+        nc.sync.dma_start(out=xs[:], in_=x_scale.rearrange("o (p t) -> p (o t)", t=4))
+        nc.sync.dma_start(out=wa_words[:].bitcast(I32), in_=attn_W_words[0].bitcast(I32))
+        load_scales(wa_scales, lambda r: attn_W_scales[0, r, :].bitcast(I32))
+        nc.sync.dma_start(out=bias_rows[32:36, :], in_=attn_b.rearrange("(c m) -> c m", m=P))
+        nc.sync.dma_start(out=bias_rows[0:16, :], in_=b_ih0.rearrange("(c m) -> c m", m=P))
+        nc.sync.dma_start(out=bias_rows[16:32, :], in_=b_hh0.rearrange("(c m) -> c m", m=P))
+        load_enc(0)
+        nc.sync.dma_start(out=xb_rest[:], in_=x_bytes[P:, :].rearrange("(i p) k -> p i k", p=P))
+        nc.sync.dma_start(out=h_rest[:], in_=h_prev[P:, :].rearrange("(i p) k -> p i k", p=P))
+        load_enc(1)
+        nc.sync.dma_start(out=wih_words[:].bitcast(I32), in_=W_ih0_words.bitcast(I32).rearrange("g p n -> p g n"))
+        nc.sync.dma_start(out=whh_words[:].bitcast(I32), in_=W_hh0_words[0].bitcast(I32))
+        load_scales(wih_scales, lambda r: W_ih0_scales[:, r, :].bitcast(I32).rearrange("g r n -> r g n"))
+        load_scales(whh_scales, lambda r: W_hh0_scales[0, r, :].bitcast(I32))
+        nc.sync.dma_start(out=c_all[:], in_=c_prev.rearrange("(i p) k -> p i k", p=P))
+
+        def prepare_biases():
+            nc.tensor.transpose(as_bf16(bank_c)[:, 0:P], bias_rows[:], ident16[:])
+            nc.scalar.copy(out=bias_cols[:], in_=as_bf16(bank_c)[:, 0:36])
+            nc.vector.tensor_tensor(out=gate_bias[:], in0=bias_cols[:, 0:16], in1=bias_cols[:, 16:32], op=ALU.add)
+            nc.vector.tensor_scalar(out=half_gate_bias[:], in0=gate_bias[:], scalar1=0.5, scalar2=None, op0=ALU.mult)
+
+        def turn_words(dst, first_col, src):
+            words = src.bitcast(F32)
+            for u in range(2):
+                nc.tensor.transpose(dst[:, first_col + u * P : first_col + (u + 1) * P], words[:, u::2], ident32[:])
+
+        def group_words(dst, src):
+            nc.scalar.copy(
+                out=dst.bitcast(F32).rearrange("p (r u) -> p r u", u=2), in_=src.rearrange("p (u r) -> p r u", u=2)
+            )
+
+        def widen_x(i):
+            src = xb_first[:] if i == 0 else xb_rest[:, i - 1, :]
+            nc.scalar.copy(out=x_wide[:], in_=src.bitcast(FP8))
+
+        def turn_xh(i):
+            turn_words(bank_a, 0, x_wide[:])
+            turn_words(bank_a, 2 * P, h_first[:] if i == 0 else h_rest[:, i - 1, :])
+
+        def scale_x():
+            nc.vector.tensor_tensor(
+                out=xh_grouped[:, 0:H].rearrange("p (r u e) -> p r u e", u=2, e=2),
+                in0=as_bf16(bank_a).rearrange("p (u r e) -> p r u e", u=2, e=2),
+                in1=xs[:].rearrange("p (u e) -> p u e", e=2).unsqueeze(1).to_broadcast([P, P, 2, 2]),
+                op=ALU.mult,
+            )
+
+        def group_h():
+            group_words(xh_grouped[:, H:], bank_a[:, 2 * P :])
+
+        def quantize_xh(i):
+            nc.vector.quantize_mx(out=xh_codes[i][:].bitcast(FP8X4), scales=xh_scales[i][:], in_=xh_grouped[:])
+
+        def mx(dst, words, scales, n, codes, code_scales, start, stop):
+            nc.tensor.matmul_mx(
+                out=dst,
+                lhsT=words[:, 2 * P * n : 2 * P * (n + 1)].bitcast(FP4X4),
+                lhsT_scale=scales[:, cols(n)],
+                rhs=codes.bitcast(FP8X4),
+                rhs_scale=code_scales,
+                start=start,
+                stop=stop,
+            )
+
+        def attn_lin(i):
+            for c in range(CHUNKS):
+                mx(bank_a[:, cols(c)], wa_words, wa_scales, c, xh_codes[i][:, 0:P], xh_scales[i][:, 0:P], True, True)
+            for c in range(CHUNKS):
+                nc.scalar.activation(
+                    out=sign_t[:, cols(c)], in_=bank_a[:, cols(c)], func=ACT.Sign, bias=bias_cols[:, 32 + c : 33 + c]
+                )
+            for c in range(CHUNKS):
+                nc.scalar.activation(
+                    out=abs_t[:, cols(c)], in_=bank_a[:, cols(c)], func=ACT.Abs, bias=bias_cols[:, 32 + c : 33 + c]
+                )
+
+        def turn(dst, src, ident):
+            for c in range(CHUNKS):
+                nc.tensor.transpose(dst[:, cols(c)], src[:, cols(c)], ident[:])
+
+        def turn_and_add(dst, terms):
+            for n, term in enumerate(terms):
+                nc.tensor.matmul(
+                    dst, lhsT=term, rhs=ident32[:], start=n == 0, stop=n == len(terms) - 1, is_transpose=True
+                )
+
+        def apply_sign(i, half):
+            ss = slice(half * S // 2, (half + 1) * S // 2)
+            nc.vector.tensor_tensor(
+                out=signed[:, ss, :],
+                in0=enc[i % 3][:, ss, :],
+                in1=as_bf16(sign_bank).unsqueeze(1).to_broadcast([P, S // 2, H]),
+                op=ALU.mult,
+            )
+
+        def max_level(n):
+            src = signed if n == 0 else level[n - 1]
+            count = S >> (n + 1)
+            for half in range(2):
+                js = slice(half * H // 2, (half + 1) * H // 2)
+                nc.vector.tensor_tensor(
+                    out=level[n][:, :, js], in0=src[:, 0:count, js], in1=src[:, count:, js], op=ALU.max
+                )
+
+        def diff(engine, largest, i, c, first=0, last=S):
+            engine.tensor_tensor(
+                out=work_of(i, c)[:, first:last, :],
+                in0=signed[:, first:last, cols(c)],
+                in1=over_s(largest[:, cols(c)], last - first),
+                op=ALU.subtract,
+            )
+
+        def score(i, c):
+            w = work_of(i, c)
+            nc.vector.tensor_tensor(out=w[:], in0=w[:], in1=over_s(abs_bank[:, cols(c)]), op=ALU.mult)
+
+        def exp(i, c):
+            w = work_of(i, c)
+            nc.scalar.activation(out=w[:], in_=w[:], func=ACT.Exp)
+
+        def weigh(engine, i, c):
+            engine.tensor_tensor(
+                out=prod_of(i, c)[:], in0=work_of(i, c)[:], in1=enc[i % 3][:, :, cols(c)], op=ALU.mult
+            )
+
+        def sum_den(i, c):
+            turn_and_add(den_bank[:, cols(c)], [work_of(i, c)[:, s, :] for s in range(S)])
+
+        def sum_num(i, c):
+            turn_and_add(num_bank[:, cols(c)], [prod_of(i, c)[:, s, :] for s in range(S)])
+
+        def invert_den():
+            nc.scalar.activation(out=log_den[:], in_=den_bank[:], func=ACT.Ln)
+            nc.scalar.activation(out=inv_den[:], in_=log_den[:], func=ACT.Exp, scale=-1.0)
+
+        def gate_sums(i, g, dst):
+            for c in range(CHUNKS):
+                n = CHUNKS * g + c
+                mx(dst[:, cols(c)], wih_words[:, 0, :], wih_scales[:, 0, :], n,
+                   xh_codes[i][:, 0:P], xh_scales[i][:, 0:P], True, False)
+                mx(dst[:, cols(c)], whh_words, whh_scales, n, xh_codes[i][:, P:], xh_scales[i][:, P:], False, False)
+                mx(dst[:, cols(c)], wih_words[:, 1, :], wih_scales[:, 1, :], n,
+                   att_codes[:], att_scales[:], False, True)
+
+        def gate_tanh(g, dst):
+            bias, scale = (gate_bias, 1.0) if g == GATE_G else (half_gate_bias, 0.5)
+            for c in range(CHUNKS):
+                n = CHUNKS * g + c
+                nc.scalar.activation(
+                    out=gate_t[g][:, cols(c)], in_=dst[:, cols(c)], func=ACT.Tanh, bias=bias[:, n : n + 1], scale=scale
+                )
+
+        def one_plus_times(dst, a, b):
+            nc.vector.scalar_tensor_tensor(out=dst, in0=a, scalar=1.0, in1=b, op0=ALU.add, op1=ALU.mult)
+
+        def cell(i):
+            for c in range(CHUNKS):
+                turn_and_add(bank_b[:, cols(c)], [keep_t[:, cols(c)], write_t[:, cols(c)]])
+            nc.scalar.activation(out=tanh_c[:], in_=bank_b[:], func=ACT.Tanh, scale=0.5)
+            nc.scalar.activation(out=c_out[i % 2][:], in_=bank_b[:], func=ACT.Copy, scale=0.5)
+            nc.sync.dma_start(out=out_1[rows(i), :], in_=c_out[i % 2][:])
+            for c in range(CHUNKS):
+                turn_and_add(bank_c[:, cols(c)], [gate_t[GATE_O][:, cols(c)], ones[:]])
+
+        def hidden(i):
+            nc.vector.scalar_tensor_tensor(
+                out=h_out[i % 2][:], in0=bank_c[:], scalar=0.5, in1=tanh_c[:], op0=ALU.mult, op1=ALU.mult
+            )
+            nc.sync.dma_start(out=out_0[rows(i), :], in_=h_out[i % 2][:])
+
+        def normalise():
+            nc.vector.tensor_tensor(out=att_t[:], in0=num_bank[:], in1=inv_den[:], op=ALU.mult)
+
+        def att_to_rows():
+            turn(as_bf16(bank_b), att_t, ident16)
+            nc.scalar.copy(out=att_rows[:], in_=as_bf16(bank_b))
+
+        def att_to_groups():
+            turn_words(bank_c, 0, att_rows[:])
+            group_words(att_grouped[:], bank_c[:, 0 : 2 * P])
+
+        def quantize_att():
+            nc.vector.quantize_mx(out=att_codes[:].bitcast(FP8X4), scales=att_scales[:], in_=att_grouped[:])
+
+        def keep_term():
+            one_plus_times(keep_t[:], gate_t[GATE_F][:], as_bf16(bank_a))
+
+        def write_term():
+            one_plus_times(write_t[:], gate_t[GATE_I][:], gate_t[GATE_G][:])
+
+        def gates(i, between):
+            gate_sums(i, GATE_F, bank_b)
+            gate_tanh(GATE_F, bank_b)
+            gate_sums(i, GATE_I, bank_a)
+            gate_tanh(GATE_I, bank_a)
+            between()
+            gate_sums(i, GATE_G, bank_c)
+            gate_tanh(GATE_G, bank_c)
+            gate_sums(i, GATE_O, bank_b)
+            gate_tanh(GATE_O, bank_b)
+            turn(as_bf16(bank_a), c_all[:, i, :], ident16)
+
+        def largest_signed(i, fillers):
+            apply_sign(i, 0)
+            apply_sign(i, 1)
+            for n in range(4):
+                max_level(n)
+                if n < len(fillers):
+                    fillers[n]()
+
+        def prepare_xh(i):
+            widen_x(i)
+            turn_xh(i)
+
+        prepare_xh(0)
+        scale_x()
+        group_h()
+        quantize_xh(0)
+        prepare_biases()
+        attn_lin(0)
+        turn(as_bf16(sign_bank), sign_t, ident16)
+        turn(abs_bank, abs_t, ident32)
+        prepare_xh(1)
+        apply_sign(0, 0)
+        apply_sign(0, 1)
+        scale_x()
+        group_h()
+        prepare_xh(2)
+        max_level(0)
+        quantize_xh(1)
+        for n in range(1, 4):
+            max_level(n)
+
+        last = TILES - 1
+        for i in range(TILES):
+            nc.tensor.matmul(max_bank[:], lhsT=ident16[:], rhs=top[:, 0, :], start=True, stop=True)
+            diff(nc.gpsimd, top[:, 0, :], i, 3, 0, GPSIMD_DIFF)
+            if i + 2 <= last:
+                scale_x()
+                group_h()
+            if i >= 3:
+                cell(i - 3)
+            diff(nc.vector, max_bank, i, 0)
+            if i + 1 <= last:
+                attn_lin(i + 1)
+            if i >= 3:
+                hidden(i - 3)
+            score(i, 0)
+            if i >= 1:
+                weigh(nc.gpsimd, i - 1, 3)
+            if i + 2 <= last:
+                load_enc(i + 2)
+
+            def sign_and_first_exp():
+                if i + 1 <= last:
+                    turn(as_bf16(sign_bank), sign_t, ident16)
+                exp(i, 0)
+
+            if i >= 2:
+                gates(i - 2, sign_and_first_exp)
+            else:
+                sign_and_first_exp()
+            diff(nc.vector, max_bank, i, 1)
+            diff(nc.vector, max_bank, i, 3, GPSIMD_DIFF, S)
+            score(i, 1)
+            sum_den(i, 0)
+            if i >= 1:
+                sum_num(i - 1, 3)
+            weigh(nc.gpsimd, i, 0)
+            exp(i, 1)
+            diff(nc.vector, max_bank, i, 2)
+            if i >= 1:
+                normalise()
+            score(i, 2)
+            sum_den(i, 1)
+            if i >= 1:
+                att_to_rows()
+            sum_num(i, 0)
+            exp(i, 2)
+            if i >= 1:
+                att_to_groups()
+            weigh(nc.gpsimd, i, 1)
+            score(i, 3)
+            if i >= 2:
+                keep_term()
+            exp(i, 3)
+            sum_den(i, 2)
+            if i == last:
+                break
+            turn(abs_bank, abs_t, ident32)
+            sum_num(i, 1)
+            weigh(nc.gpsimd, i, 2)
+            sum_den(i, 3)
+            if i + 3 <= last:
+                prepare_xh(i + 3)
+            invert_den()
+            sum_num(i, 2)
+            fillers = []
+            if i + 2 <= last:
+                fillers.append(lambda: quantize_xh(i + 2))
+            if i >= 2:
+                fillers.append(write_term)
+            if i >= 1:
+                fillers.append(quantize_att)
+            largest_signed(i + 1, fillers)
+
+        quantize_att()
+        write_term()
+        weigh(nc.vector, last, 2)
+        weigh(nc.vector, last, 3)
+        sum_num(last, 1)
+        sum_den(last, 3)
+        invert_den()
+        sum_num(last, 2)
+        cell(last - 2)
+        sum_num(last, 3)
+        hidden(last - 2)
+        normalise()
+        gates(last - 1, lambda: None)
+        keep_term()
+        write_term()
+        att_to_rows()
+        att_to_groups()
+        quantize_att()
+        cell(last - 1)
+        hidden(last - 1)
+        gates(last, lambda: None)
+        keep_term()
+        write_term()
+        cell(last)
+        hidden(last)

@@ -20,7 +20,7 @@ FP4X4 = mybir.dt.float4_e2m1fn_x4
 ACT = mybir.ActivationFunctionType
 ALU = mybir.AluOpType
 
-GPSIMD_DIFF = 13
+GPSIMD_DIFF = 7
 GATE_I, GATE_F, GATE_G, GATE_O = 0, 1, 2, 3
 
 
@@ -40,7 +40,7 @@ def tile_decoderlstm_pa_t_w4_kernel(
         def bank(name):
             return ps.tile([P, H], F32, name=name)
 
-        abs_bank, sign_bank, max_bank = bank("abs_bank"), bank("sign_bank"), bank("max_bank")
+        abs_bank, sign_max_bank, diff_bank = bank("abs_bank"), bank("sign_max_bank"), bank("diff_bank")
         den_bank, num_bank = bank("den_bank"), bank("num_bank")
         bank_a, bank_b, bank_c = bank("bank_a"), bank("bank_b"), bank("bank_c")
 
@@ -66,18 +66,22 @@ def tile_decoderlstm_pa_t_w4_kernel(
 
         enc = [sbuf("enc%d" % n, [P, S, H], BF16) for n in range(3)]
         signed = sbuf("signed", [P, S, H], BF16)
-        level = [sbuf("level%d" % n, [P, S >> (n + 1), H], BF16) for n in range(4)]
-        top = level[3]
-        work = [sbuf("work%d" % n, [P, S, P], F32) for n in range(CHUNKS + 1)]
-        prod = [sbuf("prod%d" % n, [P, S, P], F32) for n in range(3)]
+        top = sbuf("top", [P, H], BF16)
+        early_work = sbuf("early_work", [P, S, 2 * P], F32)
+        late_work = [sbuf("late_work%d" % n, [P, S, 2 * P], F32) for n in range(2)]
+        prod = [sbuf("prod%d" % n, [P, S, 2 * P], F32) for n in range(2)]
+        scratch = prod[1][:].rearrange("p s j -> p (s j)").bitcast(BF16).rearrange("p (s j) -> p s j", j=H)
+        level = [scratch[:, 0:8, :], scratch[:, 8:12, :], scratch[:, 12:14, :], top[:].unsqueeze(1)]
+        neg_top_t = sbuf("neg_top_t", [P, P], F32)
+        abs_rows = sbuf("abs_rows", [P, P], F32)
 
         x_wide = sbuf("x_wide", [P, H], BF16)
+        x_planes = sbuf("x_planes", [P, 4, P], BF16)
         xh_grouped = sbuf("xh_grouped", [P, 2 * H], BF16)
         xh_codes = [sbuf("xh_codes%d" % n, [P, 2 * P], U32) for n in range(TILES)]
         xh_scales = [sbuf("xh_scales%d" % n, [P, 2 * P], U8) for n in range(TILES)]
         abs_t = sbuf("abs_t", [P, H], F32)
         sign_t = sbuf("sign_t", [P, H], BF16)
-        log_den = sbuf("log_den", [P, H], F32)
         inv_den = sbuf("inv_den", [P, H], F32)
         att_t = sbuf("att_t", [P, H], BF16)
         att_rows = sbuf("att_rows", [P, H], BF16)
@@ -103,11 +107,15 @@ def tile_decoderlstm_pa_t_w4_kernel(
         def as_bf16(psum_tile):
             return psum_tile[:].bitcast(BF16)[:, 0:H]
 
-        def work_of(i, c):
-            return work[c + (i % 2 if c == CHUNKS - 1 else 0)]
+        sign_rows = as_bf16(sign_max_bank)
+        top_rows = sign_max_bank[:].bitcast(BF16)[:, H:]
 
-        def prod_of(i, c):
-            return prod[(CHUNKS * i + c) % 3]
+        def work_of(i, first, count=1):
+            pair = early_work if first < 2 else late_work[i % 2]
+            return pair[:, :, (first % 2) * P : (first % 2 + count) * P]
+
+        def prod_of(first, count=1):
+            return prod[first // 2][:, :, (first % 2) * P : (first % 2 + count) * P]
 
         def load_scales(plane, scales):
             for q in range(4):
@@ -169,11 +177,13 @@ def tile_decoderlstm_pa_t_w4_kernel(
             turn_words(bank_a, 2 * P, h_first[:] if i == 0 else h_rest[:, i - 1, :])
 
         def scale_x():
-            nc.vector.tensor_tensor(
-                out=xh_grouped[:, 0:H].rearrange("p (r u e) -> p r u e", u=2, e=2),
-                in0=as_bf16(bank_a).rearrange("p (u r e) -> p r u e", u=2, e=2),
-                in1=xs[:].rearrange("p (u e) -> p u e", e=2).unsqueeze(1).to_broadcast([P, P, 2, 2]),
-                op=ALU.mult,
+            turned = as_bf16(bank_a).rearrange("p (u r e) -> p u e r", u=2, e=2)
+            for t in range(4):
+                nc.scalar.activation(
+                    out=x_planes[:, t, :], in_=turned[:, t // 2, t % 2, :], func=ACT.Copy, scale=xs[:, t : t + 1]
+                )
+            nc.scalar.copy(
+                out=xh_grouped[:, 0:H].rearrange("p (r t) -> p r t", t=4), in_=x_planes[:].rearrange("p t r -> p r t")
             )
 
         def group_h():
@@ -220,7 +230,7 @@ def tile_decoderlstm_pa_t_w4_kernel(
             nc.vector.tensor_tensor(
                 out=signed[:, ss, :],
                 in0=enc[i % 3][:, ss, :],
-                in1=as_bf16(sign_bank).unsqueeze(1).to_broadcast([P, S // 2, H]),
+                in1=sign_rows.unsqueeze(1).to_broadcast([P, S // 2, H]),
                 op=ALU.mult,
             )
 
@@ -243,26 +253,52 @@ def tile_decoderlstm_pa_t_w4_kernel(
 
         def score(i, c):
             w = work_of(i, c)
-            nc.vector.tensor_tensor(out=w[:], in0=w[:], in1=over_s(abs_bank[:, cols(c)]), op=ALU.mult)
+            nc.vector.tensor_tensor(out=w, in0=w, in1=over_s(abs_bank[:, cols(c)]), op=ALU.mult)
+
+        def prepare_last_chunk():
+            staged = as_bf16(diff_bank)[:, 0:P]
+            nc.tensor.transpose(staged, top[:, cols(3)], ident16[:])
+            nc.scalar.activation(out=neg_top_t[:], in_=staged, func=ACT.Copy, scale=-1.0)
+            nc.scalar.copy(out=abs_rows[:], in_=abs_bank[:, cols(3)])
+
+        def diff_on_tensor(quarter):
+            ss = slice(4 * quarter, 4 * quarter + 4)
+            nc.tensor.matmul(diff_bank[:], lhsT=ident16[:], rhs=signed[:, ss, cols(3)], start=True, stop=False)
+            for n in range(4):
+                nc.tensor.matmul(
+                    diff_bank[:, cols(n)], lhsT=neg_top_t[:], rhs=ident32[:], start=False, stop=n == 3,
+                    is_transpose=True,
+                )
+
+        def score_from_tensor(i, quarter):
+            nc.vector.tensor_tensor(
+                out=work_of(i, 3)[:, 4 * quarter : 4 * quarter + 4, :],
+                in0=diff_bank[:].rearrange("p (s j) -> p s j", j=P),
+                in1=over_s(abs_rows[:], 4),
+                op=ALU.mult,
+            )
 
         def exp(i, c):
             w = work_of(i, c)
-            nc.scalar.activation(out=w[:], in_=w[:], func=ACT.Exp)
+            nc.scalar.activation(out=w, in_=w, func=ACT.Exp)
 
-        def weigh(engine, i, c):
+        def weigh(engine, i, first, count):
             engine.tensor_tensor(
-                out=prod_of(i, c)[:], in0=work_of(i, c)[:], in1=enc[i % 3][:, :, cols(c)], op=ALU.mult
+                out=prod_of(first, count),
+                in0=work_of(i, first, count),
+                in1=enc[i % 3][:, :, first * P : (first + count) * P],
+                op=ALU.mult,
             )
 
         def sum_den(i, c):
             turn_and_add(den_bank[:, cols(c)], [work_of(i, c)[:, s, :] for s in range(S)])
 
-        def sum_num(i, c):
-            turn_and_add(num_bank[:, cols(c)], [prod_of(i, c)[:, s, :] for s in range(S)])
+        def sum_num(c):
+            turn_and_add(num_bank[:, cols(c)], [prod_of(c)[:, s, :] for s in range(S)])
 
         def invert_den():
-            nc.scalar.activation(out=log_den[:], in_=den_bank[:], func=ACT.Ln)
-            nc.scalar.activation(out=inv_den[:], in_=log_den[:], func=ACT.Exp, scale=-1.0)
+            nc.scalar.activation(out=inv_den[:], in_=den_bank[:], func=ACT.Ln)
+            nc.scalar.activation(out=inv_den[:], in_=inv_den[:], func=ACT.Exp, scale=-1.0)
 
         def gate_sums(i, g, dst):
             for c in range(CHUNKS):
@@ -272,6 +308,18 @@ def tile_decoderlstm_pa_t_w4_kernel(
                 mx(dst[:, cols(c)], whh_words, whh_scales, n, xh_codes[i][:, P:], xh_scales[i][:, P:], False, False)
                 mx(dst[:, cols(c)], wih_words[:, 1, :], wih_scales[:, 1, :], n,
                    att_codes[:], att_scales[:], False, True)
+
+        def gate_sums_without_att(i, g, dst):
+            for c in range(CHUNKS):
+                n = CHUNKS * g + c
+                mx(dst[:, cols(c)], wih_words[:, 0, :], wih_scales[:, 0, :], n,
+                   xh_codes[i][:, 0:P], xh_scales[i][:, 0:P], c == 0, False)
+                mx(dst[:, cols(c)], whh_words, whh_scales, n, xh_codes[i][:, P:], xh_scales[i][:, P:], False, False)
+
+        def gate_sums_of_att(g, dst):
+            for c in range(CHUNKS):
+                mx(dst[:, cols(c)], wih_words[:, 1, :], wih_scales[:, 1, :], CHUNKS * g + c,
+                   att_codes[:], att_scales[:], False, c == CHUNKS - 1)
 
         def gate_tanh(g, dst):
             bias, scale = (gate_bias, 1.0) if g == GATE_G else (half_gate_bias, 0.5)
@@ -303,60 +351,42 @@ def tile_decoderlstm_pa_t_w4_kernel(
             nc.vector.tensor_tensor(out=att_t[:], in0=num_bank[:], in1=inv_den[:], op=ALU.mult)
 
         def att_to_rows():
-            turn(as_bf16(bank_b), att_t, ident16)
-            nc.scalar.copy(out=att_rows[:], in_=as_bf16(bank_b))
+            turn(as_bf16(bank_c), att_t, ident16)
+            nc.scalar.copy(out=att_rows[:], in_=as_bf16(bank_c))
 
         def att_to_groups():
-            turn_words(bank_c, 0, att_rows[:])
-            group_words(att_grouped[:], bank_c[:, 0 : 2 * P])
+            turn_words(bank_a, 0, att_rows[:])
+            group_words(att_grouped[:], bank_a[:, 0 : 2 * P])
 
         def quantize_att():
             nc.vector.quantize_mx(out=att_codes[:].bitcast(FP8X4), scales=att_scales[:], in_=att_grouped[:])
 
         def keep_term():
-            one_plus_times(keep_t[:], gate_t[GATE_F][:], as_bf16(bank_a))
+            one_plus_times(keep_t[:], gate_t[GATE_F][:], as_bf16(bank_b))
 
         def write_term():
             one_plus_times(write_t[:], gate_t[GATE_I][:], gate_t[GATE_G][:])
 
-        def gates(i, between):
-            gate_sums(i, GATE_F, bank_b)
-            gate_tanh(GATE_F, bank_b)
-            gate_sums(i, GATE_I, bank_a)
-            gate_tanh(GATE_I, bank_a)
-            between()
-            gate_sums(i, GATE_G, bank_c)
-            gate_tanh(GATE_G, bank_c)
-            gate_sums(i, GATE_O, bank_b)
-            gate_tanh(GATE_O, bank_b)
-            turn(as_bf16(bank_a), c_all[:, i, :], ident16)
+        def turn_c(i):
+            turn(as_bf16(bank_b), c_all[:, i, :], ident16)
 
-        def largest_signed(i, fillers):
-            apply_sign(i, 0)
-            apply_sign(i, 1)
-            for n in range(4):
-                max_level(n)
-                if n < len(fillers):
-                    fillers[n]()
+        def group_xh():
+            group_h()
+            scale_x()
 
-        def prepare_xh(i):
-            widen_x(i)
-            turn_xh(i)
-
-        prepare_xh(0)
-        scale_x()
-        group_h()
+        widen_x(0)
+        turn_xh(0)
+        group_xh()
         quantize_xh(0)
         prepare_biases()
         attn_lin(0)
-        turn(as_bf16(sign_bank), sign_t, ident16)
+        turn(sign_rows, sign_t, ident16)
         turn(abs_bank, abs_t, ident32)
-        prepare_xh(1)
+        widen_x(1)
+        turn_xh(1)
+        group_xh()
         apply_sign(0, 0)
         apply_sign(0, 1)
-        scale_x()
-        group_h()
-        prepare_xh(2)
         max_level(0)
         quantize_xh(1)
         for n in range(1, 4):
@@ -364,68 +394,83 @@ def tile_decoderlstm_pa_t_w4_kernel(
 
         last = TILES - 1
         for i in range(TILES):
-            nc.tensor.matmul(max_bank[:], lhsT=ident16[:], rhs=top[:, 0, :], start=True, stop=True)
-            diff(nc.gpsimd, top[:, 0, :], i, 3, 0, GPSIMD_DIFF)
-            if i + 2 <= last:
-                scale_x()
-                group_h()
+            nc.tensor.matmul(top_rows, lhsT=ident16[:], rhs=top[:], start=True, stop=True)
+            if i == 0:
+                diff(nc.gpsimd, top, i, 1)
+            on_gpsimd = S if i == 0 else GPSIMD_DIFF
+            diff(nc.gpsimd, top, i, 2, 0, on_gpsimd)
+            prepare_last_chunk()
             if i >= 3:
+                keep_term()
                 cell(i - 3)
-            diff(nc.vector, max_bank, i, 0)
+            diff(nc.vector, top_rows, i, 0)
             if i + 1 <= last:
                 attn_lin(i + 1)
-            if i >= 3:
-                hidden(i - 3)
-            score(i, 0)
             if i >= 1:
-                weigh(nc.gpsimd, i - 1, 3)
+                diff(nc.vector, top_rows, i, 1)
+                weigh(nc.gpsimd, i - 1, 2, 2)
             if i + 2 <= last:
                 load_enc(i + 2)
-
-            def sign_and_first_exp():
-                if i + 1 <= last:
-                    turn(as_bf16(sign_bank), sign_t, ident16)
-                exp(i, 0)
-
+            score(i, 0)
+            diff_on_tensor(0)
             if i >= 2:
-                gates(i - 2, sign_and_first_exp)
-            else:
-                sign_and_first_exp()
-            diff(nc.vector, max_bank, i, 1)
-            diff(nc.vector, max_bank, i, 3, GPSIMD_DIFF, S)
+                for g, dst in ((GATE_F, bank_b), (GATE_I, bank_a)):
+                    gate_sums(i - 2, g, dst)
+                    gate_tanh(g, dst)
+                gate_sums(i - 2, GATE_G, bank_b)
+                gate_sums(i - 2, GATE_O, bank_a)
+            if i + 2 <= last:
+                widen_x(i + 2)
+            exp(i, 0)
             score(i, 1)
-            sum_den(i, 0)
-            if i >= 1:
-                sum_num(i - 1, 3)
-            weigh(nc.gpsimd, i, 0)
             exp(i, 1)
-            diff(nc.vector, max_bank, i, 2)
-            if i >= 1:
-                normalise()
-            score(i, 2)
-            sum_den(i, 1)
-            if i >= 1:
-                att_to_rows()
-            sum_num(i, 0)
-            exp(i, 2)
-            if i >= 1:
-                att_to_groups()
-            weigh(nc.gpsimd, i, 1)
-            score(i, 3)
             if i >= 2:
-                keep_term()
-            exp(i, 3)
-            sum_den(i, 2)
+                gate_tanh(GATE_G, bank_b)
+                gate_tanh(GATE_O, bank_a)
+            score_from_tensor(i, 0)
+            diff_on_tensor(1)
+            sum_den(i, 0)
+            if i >= 3:
+                hidden(i - 3)
+            if on_gpsimd < S:
+                diff(nc.vector, top_rows, i, 2, on_gpsimd, S)
+            score_from_tensor(i, 1)
+            diff_on_tensor(2)
+            if i >= 1:
+                sum_num(2)
+            weigh(nc.gpsimd, i, 0, 1 if i == last else 2)
+            score(i, 2)
+            if i + 1 <= last:
+                turn(sign_rows, sign_t, ident16)
+            if i + 2 <= last:
+                turn_xh(i + 2)
+            exp(i, 2)
+            if i + 2 <= last:
+                group_xh()
+            score_from_tensor(i, 2)
+            diff_on_tensor(3)
+            if i >= 1:
+                sum_num(3)
             if i == last:
                 break
+            apply_sign(i + 1, 0)
+            score_from_tensor(i, 3)
+            exp(i, 3)
+            sum_den(i, 1)
+            if i >= 1:
+                normalise()
+                att_to_rows()
+            apply_sign(i + 1, 1)
+            sum_den(i, 2)
+            if i >= 1:
+                att_to_groups()
             turn(abs_bank, abs_t, ident32)
-            sum_num(i, 1)
-            weigh(nc.gpsimd, i, 2)
+            if i >= 2:
+                turn_c(i - 2)
             sum_den(i, 3)
-            if i + 3 <= last:
-                prepare_xh(i + 3)
             invert_den()
-            sum_num(i, 2)
+            sum_num(0)
+            sum_num(1)
             fillers = []
             if i + 2 <= last:
                 fillers.append(lambda: quantize_xh(i + 2))
@@ -433,29 +478,58 @@ def tile_decoderlstm_pa_t_w4_kernel(
                 fillers.append(write_term)
             if i >= 1:
                 fillers.append(quantize_att)
-            largest_signed(i + 1, fillers)
+            for n in range(4):
+                max_level(n)
+                if n < len(fillers):
+                    fillers[n]()
 
-        quantize_att()
-        write_term()
-        weigh(nc.vector, last, 2)
-        weigh(nc.vector, last, 3)
-        sum_num(last, 1)
-        sum_den(last, 3)
-        invert_den()
-        sum_num(last, 2)
-        cell(last - 2)
-        sum_num(last, 3)
-        hidden(last - 2)
+        tail_banks = ((GATE_F, sign_max_bank), (GATE_I, abs_bank), (GATE_G, diff_bank), (GATE_O, den_bank))
+        score_from_tensor(last, 3)
+        exp(last, 3)
         normalise()
-        gates(last - 1, lambda: None)
+        att_to_rows()
+        turn_c(last - 2)
+        sum_den(last, 1)
+        weigh(nc.vector, last, 1, 1)
+        att_to_groups()
+        sum_den(last, 2)
         keep_term()
         write_term()
-        att_to_rows()
-        att_to_groups()
         quantize_att()
+        sum_den(last, 3)
+        weigh(nc.vector, last, 2, 1)
+        weigh(nc.vector, last, 3, 1)
+        invert_den()
+        sum_num(0)
+        sum_num(1)
+        cell(last - 2)
+        sum_num(2)
+        for g, dst in tail_banks[:2]:
+            gate_sums(last - 1, g, dst)
+        hidden(last - 2)
+        sum_num(3)
+        normalise()
+        for g, dst in tail_banks[:2]:
+            gate_tanh(g, dst)
+        gate_sums(last - 1, *tail_banks[2])
+        att_to_rows()
+        gate_sums(last - 1, *tail_banks[3])
+        turn_c(last - 1)
+        gate_tanh(*tail_banks[2])
+        att_to_groups()
+        keep_term()
+        quantize_att()
+        write_term()
+        gate_tanh(*tail_banks[3])
+        gate_sums(last, *tail_banks[0])
+        gate_sums(last, *tail_banks[1])
         cell(last - 1)
+        gate_sums(last, *tail_banks[2])
+        turn_c(last)
+        gate_sums(last, *tail_banks[3])
         hidden(last - 1)
-        gates(last, lambda: None)
+        for g, dst in tail_banks:
+            gate_tanh(g, dst)
         keep_term()
         write_term()
         cell(last)

@@ -20,7 +20,8 @@ FP4X4 = mybir.dt.float4_e2m1fn_x4
 ACT = mybir.ActivationFunctionType
 ALU = mybir.AluOpType
 
-GPSIMD_DIFF = 7
+GPSIMD_DIFF = 11
+HALF = S // 2
 GATE_I, GATE_F, GATE_G, GATE_O = 0, 1, 2, 3
 
 
@@ -40,13 +41,13 @@ def tile_decoderlstm_pa_t_w4_kernel(
         def bank(name):
             return ps.tile([P, H], F32, name=name)
 
-        abs_bank, sign_max_bank, diff_bank = bank("abs_bank"), bank("sign_max_bank"), bank("diff_bank")
+        abs_bank, sign_bank, top_bank = bank("abs_bank"), bank("sign_bank"), bank("top_bank")
         den_bank, num_bank = bank("den_bank"), bank("num_bank")
         bank_a, bank_b, bank_c = bank("bank_a"), bank("bank_b"), bank("bank_c")
 
         ident32 = sbuf("ident32", [P, P], F32)
         ident16 = sbuf("ident16", [P, P], BF16)
-        ones = sbuf("ones", [P, P], F32)
+        ones = sbuf("ones", [P, H], BF16)
         bias_rows = sbuf("bias_rows", [P, P], BF16)
         bias_cols = sbuf("bias_cols", [P, 36], F32)
         gate_bias = sbuf("gate_bias", [P, 16], F32)
@@ -72,8 +73,6 @@ def tile_decoderlstm_pa_t_w4_kernel(
         prod = [sbuf("prod%d" % n, [P, S, 2 * P], F32) for n in range(2)]
         scratch = prod[1][:].rearrange("p s j -> p (s j)").bitcast(BF16).rearrange("p (s j) -> p s j", j=H)
         level = [scratch[:, 0:8, :], scratch[:, 8:12, :], scratch[:, 12:14, :], top[:].unsqueeze(1)]
-        neg_top_t = sbuf("neg_top_t", [P, P], F32)
-        abs_rows = sbuf("abs_rows", [P, P], F32)
 
         x_wide = sbuf("x_wide", [P, H], BF16)
         x_planes = sbuf("x_planes", [P, 4, P], BF16)
@@ -107,8 +106,7 @@ def tile_decoderlstm_pa_t_w4_kernel(
         def as_bf16(psum_tile):
             return psum_tile[:].bitcast(BF16)[:, 0:H]
 
-        sign_rows = as_bf16(sign_max_bank)
-        top_rows = sign_max_bank[:].bitcast(BF16)[:, H:]
+        sign_rows = as_bf16(sign_bank)
 
         def work_of(i, first, count=1):
             pair = early_work if first < 2 else late_work[i % 2]
@@ -215,9 +213,13 @@ def tile_decoderlstm_pa_t_w4_kernel(
                     out=abs_t[:, cols(c)], in_=bank_a[:, cols(c)], func=ACT.Abs, bias=bias_cols[:, 32 + c : 33 + c]
                 )
 
-        def turn(dst, src, ident):
+        def turn_bf16(dst, src):
             for c in range(CHUNKS):
-                nc.tensor.transpose(dst[:, cols(c)], src[:, cols(c)], ident[:])
+                nc.tensor.matmul(dst[:, cols(c)], lhsT=src[:, cols(c)], rhs=ident16[:], start=True, stop=True)
+
+        def turn_abs():
+            for c in range(CHUNKS):
+                nc.tensor.transpose(abs_bank[:, cols(c)], abs_t[:, cols(c)], ident32[:])
 
         def turn_and_add(dst, terms):
             for n, term in enumerate(terms):
@@ -255,29 +257,6 @@ def tile_decoderlstm_pa_t_w4_kernel(
             w = work_of(i, c)
             nc.vector.tensor_tensor(out=w, in0=w, in1=over_s(abs_bank[:, cols(c)]), op=ALU.mult)
 
-        def prepare_last_chunk():
-            staged = as_bf16(diff_bank)[:, 0:P]
-            nc.tensor.transpose(staged, top[:, cols(3)], ident16[:])
-            nc.scalar.activation(out=neg_top_t[:], in_=staged, func=ACT.Copy, scale=-1.0)
-            nc.scalar.copy(out=abs_rows[:], in_=abs_bank[:, cols(3)])
-
-        def diff_on_tensor(quarter):
-            ss = slice(4 * quarter, 4 * quarter + 4)
-            nc.tensor.matmul(diff_bank[:], lhsT=ident16[:], rhs=signed[:, ss, cols(3)], start=True, stop=False)
-            for n in range(4):
-                nc.tensor.matmul(
-                    diff_bank[:, cols(n)], lhsT=neg_top_t[:], rhs=ident32[:], start=False, stop=n == 3,
-                    is_transpose=True,
-                )
-
-        def score_from_tensor(i, quarter):
-            nc.vector.tensor_tensor(
-                out=work_of(i, 3)[:, 4 * quarter : 4 * quarter + 4, :],
-                in0=diff_bank[:].rearrange("p (s j) -> p s j", j=P),
-                in1=over_s(abs_rows[:], 4),
-                op=ALU.mult,
-            )
-
         def exp(i, c):
             w = work_of(i, c)
             nc.scalar.activation(out=w, in_=w, func=ACT.Exp)
@@ -290,11 +269,16 @@ def tile_decoderlstm_pa_t_w4_kernel(
                 op=ALU.mult,
             )
 
-        def sum_den(i, c):
-            turn_and_add(den_bank[:, cols(c)], [work_of(i, c)[:, s, :] for s in range(S)])
+        def fold(terms, count):
+            nc.vector.tensor_tensor(
+                out=terms[:, 0:count, :], in0=terms[:, 0:count, :], in1=terms[:, count : 2 * count, :], op=ALU.add
+            )
 
-        def sum_num(c):
-            turn_and_add(num_bank[:, cols(c)], [prod_of(c)[:, s, :] for s in range(S)])
+        def sum_den(i, c, count=S):
+            turn_and_add(den_bank[:, cols(c)], [work_of(i, c)[:, s, :] for s in range(count)])
+
+        def sum_num(c, count=S):
+            turn_and_add(num_bank[:, cols(c)], [prod_of(c)[:, s, :] for s in range(count)])
 
         def invert_den():
             nc.scalar.activation(out=inv_den[:], in_=den_bank[:], func=ACT.Ln)
@@ -338,8 +322,12 @@ def tile_decoderlstm_pa_t_w4_kernel(
             nc.scalar.activation(out=tanh_c[:], in_=bank_b[:], func=ACT.Tanh, scale=0.5)
             nc.scalar.activation(out=c_out[i % 2][:], in_=bank_b[:], func=ACT.Copy, scale=0.5)
             nc.sync.dma_start(out=out_1[rows(i), :], in_=c_out[i % 2][:])
+            nc.tensor.matmul(bank_c[:], lhsT=ident16[:], rhs=ones[:], start=True, stop=False)
             for c in range(CHUNKS):
-                turn_and_add(bank_c[:, cols(c)], [gate_t[GATE_O][:, cols(c)], ones[:]])
+                nc.tensor.matmul(
+                    bank_c[:, cols(c)], lhsT=gate_t[GATE_O][:, cols(c)], rhs=ident32[:], start=False,
+                    stop=c == CHUNKS - 1, is_transpose=True,
+                )
 
         def hidden(i):
             nc.vector.scalar_tensor_tensor(
@@ -350,25 +338,25 @@ def tile_decoderlstm_pa_t_w4_kernel(
         def normalise():
             nc.vector.tensor_tensor(out=att_t[:], in0=num_bank[:], in1=inv_den[:], op=ALU.mult)
 
-        def att_to_rows():
-            turn(as_bf16(bank_c), att_t, ident16)
-            nc.scalar.copy(out=att_rows[:], in_=as_bf16(bank_c))
+        def att_to_rows(dst):
+            turn_bf16(as_bf16(dst), att_t)
+            nc.scalar.copy(out=att_rows[:], in_=as_bf16(dst))
 
-        def att_to_groups():
-            turn_words(bank_a, 0, att_rows[:])
-            group_words(att_grouped[:], bank_a[:, 0 : 2 * P])
+        def att_to_groups(dst):
+            turn_words(dst, 0, att_rows[:])
+            group_words(att_grouped[:], dst[:, 0 : 2 * P])
 
         def quantize_att():
             nc.vector.quantize_mx(out=att_codes[:].bitcast(FP8X4), scales=att_scales[:], in_=att_grouped[:])
 
-        def keep_term():
-            one_plus_times(keep_t[:], gate_t[GATE_F][:], as_bf16(bank_b))
+        def keep_term(src):
+            one_plus_times(keep_t[:], gate_t[GATE_F][:], as_bf16(src))
 
         def write_term():
             one_plus_times(write_t[:], gate_t[GATE_I][:], gate_t[GATE_G][:])
 
-        def turn_c(i):
-            turn(as_bf16(bank_b), c_all[:, i, :], ident16)
+        def turn_c(i, dst):
+            turn_bf16(as_bf16(dst), c_all[:, i, :])
 
         def group_xh():
             group_h()
@@ -380,11 +368,12 @@ def tile_decoderlstm_pa_t_w4_kernel(
         quantize_xh(0)
         prepare_biases()
         attn_lin(0)
-        turn(sign_rows, sign_t, ident16)
-        turn(abs_bank, abs_t, ident32)
+        turn_bf16(sign_rows, sign_t)
+        turn_abs()
         widen_x(1)
         turn_xh(1)
         group_xh()
+        widen_x(2)
         apply_sign(0, 0)
         apply_sign(0, 1)
         max_level(0)
@@ -393,84 +382,90 @@ def tile_decoderlstm_pa_t_w4_kernel(
             max_level(n)
 
         last = TILES - 1
-        for i in range(TILES):
-            nc.tensor.matmul(top_rows, lhsT=ident16[:], rhs=top[:], start=True, stop=True)
+
+        def spread_top(half):
+            js = slice(half * H // 2, (half + 1) * H // 2)
+            nc.tensor.matmul(top_bank[:, js], lhsT=ident16[:], rhs=top[:, js], start=True, stop=True)
+
+        for i in range(last):
+            spread_top(0)
             if i == 0:
                 diff(nc.gpsimd, top, i, 1)
             on_gpsimd = S if i == 0 else GPSIMD_DIFF
-            diff(nc.gpsimd, top, i, 2, 0, on_gpsimd)
-            prepare_last_chunk()
+            diff(nc.gpsimd, top, i, 3, 0, on_gpsimd)
             if i >= 3:
-                keep_term()
+                keep_term(bank_b)
+            diff(nc.vector, top_bank, i, 0)
+            attn_lin(i + 1)
+            if i >= 2:
+                gate_sums(i - 2, GATE_I, sign_bank)
+                gate_tanh(GATE_I, sign_bank)
+            if i >= 3:
                 cell(i - 3)
-            diff(nc.vector, top_rows, i, 0)
-            if i + 1 <= last:
-                attn_lin(i + 1)
+            if i + 2 <= last:
+                turn_xh(i + 2)
+                group_xh()
             if i >= 1:
-                diff(nc.vector, top_rows, i, 1)
+                diff(nc.vector, top_bank, i, 1)
                 weigh(nc.gpsimd, i - 1, 2, 2)
+                sum_num(0)
             if i + 2 <= last:
                 load_enc(i + 2)
-            score(i, 0)
-            diff_on_tensor(0)
             if i >= 2:
-                for g, dst in ((GATE_F, bank_b), (GATE_I, bank_a)):
-                    gate_sums(i - 2, g, dst)
-                    gate_tanh(g, dst)
                 gate_sums(i - 2, GATE_G, bank_b)
-                gate_sums(i - 2, GATE_O, bank_a)
-            if i + 2 <= last:
-                widen_x(i + 2)
+            spread_top(1)
+            if i >= 1:
+                sum_num(1)
+                sum_den(i - 1, 2)
+                sum_den(i - 1, 3)
+            score(i, 0)
             exp(i, 0)
             score(i, 1)
             exp(i, 1)
-            if i >= 2:
-                gate_tanh(GATE_G, bank_b)
-                gate_tanh(GATE_O, bank_a)
-            score_from_tensor(i, 0)
-            diff_on_tensor(1)
-            sum_den(i, 0)
             if i >= 3:
                 hidden(i - 3)
-            if on_gpsimd < S:
-                diff(nc.vector, top_rows, i, 2, on_gpsimd, S)
-            score_from_tensor(i, 1)
-            diff_on_tensor(2)
+            if i >= 2:
+                gate_tanh(GATE_G, bank_b)
+            if i >= 1:
+                invert_den()
+            turn_bf16(sign_rows, sign_t)
+            diff(nc.vector, top_bank, i, 2)
+            if i >= 1:
+                diff(nc.vector, top_bank, i, 3, on_gpsimd, S)
+            if i == 0:
+                weigh(nc.gpsimd, i, 0, 1)
+                weigh(nc.gpsimd, i, 1, 1)
+            else:
+                weigh(nc.gpsimd, i, 0, 2)
+            if i >= 2:
+                gate_sums(i - 2, GATE_F, bank_a)
+            score(i, 2)
+            exp(i, 2)
+            if i >= 2:
+                gate_tanh(GATE_F, bank_a)
+            score(i, 3)
             if i >= 1:
                 sum_num(2)
-            weigh(nc.gpsimd, i, 0, 1 if i == last else 2)
-            score(i, 2)
-            if i + 1 <= last:
-                turn(sign_rows, sign_t, ident16)
-            if i + 2 <= last:
-                turn_xh(i + 2)
-            exp(i, 2)
-            if i + 2 <= last:
-                group_xh()
-            score_from_tensor(i, 2)
-            diff_on_tensor(3)
-            if i >= 1:
                 sum_num(3)
-            if i == last:
-                break
-            apply_sign(i + 1, 0)
-            score_from_tensor(i, 3)
+            if i >= 2:
+                gate_sums(i - 2, GATE_O, bank_b)
             exp(i, 3)
-            sum_den(i, 1)
+            sum_den(i, 0)
+            apply_sign(i + 1, 0)
+            apply_sign(i + 1, 1)
+            turn_abs()
             if i >= 1:
                 normalise()
-                att_to_rows()
-            apply_sign(i + 1, 1)
-            sum_den(i, 2)
-            if i >= 1:
-                att_to_groups()
-            turn(abs_bank, abs_t, ident32)
+                att_to_rows(bank_c)
             if i >= 2:
-                turn_c(i - 2)
-            sum_den(i, 3)
-            invert_den()
-            sum_num(0)
-            sum_num(1)
+                gate_tanh(GATE_O, bank_b)
+            sum_den(i, 1)
+            if i >= 1:
+                att_to_groups(bank_a)
+            if i >= 2:
+                turn_c(i - 2, bank_b)
+            if i + 3 <= last:
+                widen_x(i + 3)
             fillers = []
             if i + 2 <= last:
                 fillers.append(lambda: quantize_xh(i + 2))
@@ -479,58 +474,98 @@ def tile_decoderlstm_pa_t_w4_kernel(
             if i >= 1:
                 fillers.append(quantize_att)
             for n in range(4):
+                if n == 3 and fillers:
+                    fillers.pop()()
                 max_level(n)
-                if n < len(fillers):
-                    fillers[n]()
+                if n < 2 and len(fillers) > 1:
+                    fillers.pop(0)()
 
-        tail_banks = ((GATE_F, sign_max_bank), (GATE_I, abs_bank), (GATE_G, diff_bank), (GATE_O, den_bank))
-        score_from_tensor(last, 3)
-        exp(last, 3)
-        normalise()
-        att_to_rows()
-        turn_c(last - 2)
-        sum_den(last, 1)
-        weigh(nc.vector, last, 1, 1)
-        att_to_groups()
-        sum_den(last, 2)
-        keep_term()
-        write_term()
-        quantize_att()
-        sum_den(last, 3)
-        weigh(nc.vector, last, 2, 1)
-        weigh(nc.vector, last, 3, 1)
+        held = ((GATE_F, bank_a), (GATE_I, sign_bank), (GATE_G, top_bank), (GATE_O, abs_bank))
+        spread_top(0)
+        diff(nc.gpsimd, top, last, 3, 0, GPSIMD_DIFF)
+        keep_term(bank_b)
+        diff(nc.vector, top_bank, last, 0)
+        for g, dst in ((GATE_I, sign_bank), (GATE_G, bank_a)):
+            gate_sums(last - 2, g, dst)
+            gate_tanh(g, dst)
+        sum_den(last - 1, 2)
+        sum_den(last - 1, 3)
         invert_den()
+        diff(nc.vector, top_bank, last, 1)
+        weigh(nc.gpsimd, last - 1, 2, 2)
+        spread_top(1)
         sum_num(0)
+        gate_sums(last - 2, GATE_F, sign_bank)
+        gate_sums(last - 2, GATE_O, bank_a)
         sum_num(1)
-        cell(last - 2)
+        score(last, 0)
+        exp(last, 0)
+        score(last, 1)
+        exp(last, 1)
+        diff(nc.vector, top_bank, last, 2)
+        diff(nc.vector, top_bank, last, 3, GPSIMD_DIFF, S)
+        weigh(nc.gpsimd, last, 0, 1)
         sum_num(2)
-        for g, dst in tail_banks[:2]:
-            gate_sums(last - 1, g, dst)
-        hidden(last - 2)
+        cell(last - 3)
+        gate_tanh(GATE_F, sign_bank)
+        gate_tanh(GATE_O, bank_a)
+        gate_sums_without_att(last - 1, *held[2])
         sum_num(3)
+        score(last, 2)
+        exp(last, 2)
+        score(last, 3)
+        exp(last, 3)
+        weigh(nc.vector, last, 1, 1)
+        hidden(last - 3)
         normalise()
-        for g, dst in tail_banks[:2]:
-            gate_tanh(g, dst)
-        gate_sums(last - 1, *tail_banks[2])
-        att_to_rows()
-        gate_sums(last - 1, *tail_banks[3])
-        turn_c(last - 1)
-        gate_tanh(*tail_banks[2])
-        att_to_groups()
-        keep_term()
-        quantize_att()
+        gate_sums_without_att(last - 1, *held[1])
+        sum_den(last, 0)
+        att_to_rows(bank_c)
+        gate_sums_without_att(last - 1, *held[0])
+        turn_c(last - 2, bank_b)
+        sum_den(last, 1)
+        att_to_groups(bank_c)
+        gate_sums_without_att(last - 1, *held[3])
+        sum_den(last, 2)
+        fold(prod_of(0, 2), HALF)
+        weigh(nc.vector, last, 2, 1)
         write_term()
-        gate_tanh(*tail_banks[3])
-        gate_sums(last, *tail_banks[0])
-        gate_sums(last, *tail_banks[1])
-        cell(last - 1)
-        gate_sums(last, *tail_banks[2])
-        turn_c(last)
-        gate_sums(last, *tail_banks[3])
-        hidden(last - 1)
-        for g, dst in tail_banks:
+        keep_term(bank_b)
+        quantize_att()
+        weigh(nc.vector, last, 3, 1)
+        fold(prod_of(2, 2), HALF)
+        sum_den(last, 3)
+        invert_den()
+        for g, dst in held:
+            gate_sums_of_att(g, dst)
+        sum_num(0, HALF)
+        sum_num(1, HALF)
+        cell(last - 2)
+        hidden(last - 2)
+        for g, dst in held[:3]:
             gate_tanh(g, dst)
-        keep_term()
+        sum_num(2, HALF)
+        sum_num(3, HALF)
+        normalise()
+        gate_sums_without_att(last, *held[0])
+        att_to_rows(bank_c)
+        turn_c(last - 1, bank_b)
+        write_term()
+        keep_term(bank_b)
+        gate_tanh(*held[3])
+        gate_sums_without_att(last, *held[1])
+        att_to_groups(bank_c)
+        quantize_att()
+        gate_sums_without_att(last, *held[2])
+        gate_sums_without_att(last, *held[3])
+        cell(last - 1)
+        for g, dst in held:
+            gate_sums_of_att(g, dst)
+        hidden(last - 1)
+        turn_c(last, bank_b)
+        for g, dst in held:
+            gate_tanh(g, dst)
+        keep_term(bank_b)
         write_term()
         cell(last)
         hidden(last)

@@ -73,6 +73,8 @@ def tile_decoderlstm_pa_t_w4_kernel(
         prod = [sbuf("prod%d" % n, [P, S, 2 * P], F32) for n in range(2)]
         scratch = prod[1][:].rearrange("p s j -> p (s j)").bitcast(BF16).rearrange("p (s j) -> p s j", j=H)
         level = [scratch[:, 0:8, :], scratch[:, 8:12, :], scratch[:, 12:14, :], top[:].unsqueeze(1)]
+        spare = prod[0][:].rearrange("p s j -> p (s j)").bitcast(BF16).rearrange("p (s j) -> p s j", j=H)
+        low_level = [spare[:, 0:8, :], spare[:, 8:12, :], spare[:, 12:14, :], spare[:, 14:15, :]]
 
         x_wide = sbuf("x_wide", [P, H], BF16)
         x_planes = sbuf("x_planes", [P, 4, P], BF16)
@@ -119,9 +121,9 @@ def tile_decoderlstm_pa_t_w4_kernel(
             for q in range(4):
                 nc.sync.dma_start(out=plane[32 * q : 32 * q + 4].bitcast(I32), in_=scales(slice(4 * q, 4 * q + 4)))
 
-        def load_enc(i):
-            for half in range(2):
-                ss = slice(half * S // 2, (half + 1) * S // 2)
+        def load_enc(i, parts=2):
+            for part in range(parts):
+                ss = slice(part * S // parts, (part + 1) * S // parts)
                 nc.sync.dma_start(out=enc[i % 3][:, ss, :], in_=enc_seq[ss, rows(i), :].rearrange("s b j -> b s j"))
 
         nc.gpsimd.memset(wa_scales[:].bitcast(I32), 0)
@@ -136,11 +138,11 @@ def tile_decoderlstm_pa_t_w4_kernel(
         nc.sync.dma_start(out=h_first[:], in_=h_prev[rows(0), :])
         nc.sync.dma_start(out=xs[:], in_=x_scale.rearrange("o (p t) -> p (o t)", t=4))
         nc.sync.dma_start(out=wa_words[:].bitcast(I32), in_=attn_W_words[0].bitcast(I32))
+        load_enc(0, 4)
         load_scales(wa_scales, lambda r: attn_W_scales[0, r, :].bitcast(I32))
         nc.sync.dma_start(out=bias_rows[32:36, :], in_=attn_b.rearrange("(c m) -> c m", m=P))
         nc.sync.dma_start(out=bias_rows[0:16, :], in_=b_ih0.rearrange("(c m) -> c m", m=P))
         nc.sync.dma_start(out=bias_rows[16:32, :], in_=b_hh0.rearrange("(c m) -> c m", m=P))
-        load_enc(0)
         nc.sync.dma_start(out=xb_rest[:], in_=x_bytes[P:, :].rearrange("(i p) k -> p i k", p=P))
         nc.sync.dma_start(out=h_rest[:], in_=h_prev[P:, :].rearrange("(i p) k -> p i k", p=P))
         load_enc(1)
@@ -153,6 +155,8 @@ def tile_decoderlstm_pa_t_w4_kernel(
         def prepare_biases():
             nc.tensor.transpose(as_bf16(bank_c)[:, 0:P], bias_rows[:], ident16[:])
             nc.scalar.copy(out=bias_cols[:], in_=as_bf16(bank_c)[:, 0:36])
+
+        def add_gate_biases():
             nc.vector.tensor_tensor(out=gate_bias[:], in0=bias_cols[:, 0:16], in1=bias_cols[:, 16:32], op=ALU.add)
             nc.vector.tensor_scalar(out=half_gate_bias[:], in0=gate_bias[:], scalar1=0.5, scalar2=None, op0=ALU.mult)
 
@@ -210,7 +214,7 @@ def tile_decoderlstm_pa_t_w4_kernel(
                 )
             for c in range(CHUNKS):
                 nc.scalar.activation(
-                    out=abs_t[:, cols(c)], in_=bank_a[:, cols(c)], func=ACT.Abs, bias=bias_cols[:, 32 + c : 33 + c]
+                    out=abs_t[:, cols(c)], in_=bank_a[:, cols(c)], func=ACT.Identity if i == 0 else ACT.Abs, bias=bias_cols[:, 32 + c : 33 + c]
                 )
 
         def turn_bf16(dst, src):
@@ -248,7 +252,7 @@ def tile_decoderlstm_pa_t_w4_kernel(
         def diff(engine, largest, i, c, first=0, last=S):
             engine.tensor_tensor(
                 out=work_of(i, c)[:, first:last, :],
-                in0=signed[:, first:last, cols(c)],
+                in0=(enc[0] if i == 0 else signed)[:, first:last, cols(c)],
                 in1=over_s(largest[:, cols(c)], last - first),
                 op=ALU.subtract,
             )
@@ -261,11 +265,11 @@ def tile_decoderlstm_pa_t_w4_kernel(
             w = work_of(i, c)
             nc.scalar.activation(out=w, in_=w, func=ACT.Exp)
 
-        def weigh(engine, i, first, count):
+        def weigh(engine, i, first, count, ss=slice(0, S)):
             engine.tensor_tensor(
-                out=prod_of(first, count),
-                in0=work_of(i, first, count),
-                in1=enc[i % 3][:, :, first * P : (first + count) * P],
+                out=prod_of(first, count)[:, ss, :],
+                in0=work_of(i, first, count)[:, ss, :],
+                in1=enc[i % 3][:, ss, first * P : (first + count) * P],
                 op=ALU.mult,
             )
 
@@ -316,22 +320,22 @@ def tile_decoderlstm_pa_t_w4_kernel(
         def one_plus_times(dst, a, b):
             nc.vector.scalar_tensor_tensor(out=dst, in0=a, scalar=1.0, in1=b, op0=ALU.add, op1=ALU.mult)
 
-        def cell(i):
+        def cell(i, c_bank=bank_b, o_bank=bank_c):
             for c in range(CHUNKS):
-                turn_and_add(bank_b[:, cols(c)], [keep_t[:, cols(c)], write_t[:, cols(c)]])
-            nc.scalar.activation(out=tanh_c[:], in_=bank_b[:], func=ACT.Tanh, scale=0.5)
-            nc.scalar.activation(out=c_out[i % 2][:], in_=bank_b[:], func=ACT.Copy, scale=0.5)
+                turn_and_add(c_bank[:, cols(c)], [keep_t[:, cols(c)], write_t[:, cols(c)]])
+            nc.scalar.activation(out=tanh_c[:], in_=c_bank[:], func=ACT.Tanh, scale=0.5)
+            nc.scalar.activation(out=c_out[i % 2][:], in_=c_bank[:], func=ACT.Copy, scale=0.5)
             nc.sync.dma_start(out=out_1[rows(i), :], in_=c_out[i % 2][:])
-            nc.tensor.matmul(bank_c[:], lhsT=ident16[:], rhs=ones[:], start=True, stop=False)
+            nc.tensor.matmul(o_bank[:], lhsT=ident16[:], rhs=ones[:], start=True, stop=False)
             for c in range(CHUNKS):
                 nc.tensor.matmul(
-                    bank_c[:, cols(c)], lhsT=gate_t[GATE_O][:, cols(c)], rhs=ident32[:], start=False,
+                    o_bank[:, cols(c)], lhsT=gate_t[GATE_O][:, cols(c)], rhs=ident32[:], start=False,
                     stop=c == CHUNKS - 1, is_transpose=True,
                 )
 
-        def hidden(i):
+        def hidden(i, o_bank=bank_c):
             nc.vector.scalar_tensor_tensor(
-                out=h_out[i % 2][:], in0=bank_c[:], scalar=0.5, in1=tanh_c[:], op0=ALU.mult, op1=ALU.mult
+                out=h_out[i % 2][:], in0=o_bank[:], scalar=0.5, in1=tanh_c[:], op0=ALU.mult, op1=ALU.mult
             )
             nc.sync.dma_start(out=out_0[rows(i), :], in_=h_out[i % 2][:])
 
@@ -362,10 +366,27 @@ def tile_decoderlstm_pa_t_w4_kernel(
             group_h()
             scale_x()
 
+        def extremes(src, dst, count, first=0):
+            for levels, op in ((level, ALU.max), (low_level, ALU.min)):
+                values = enc[0] if src is None else levels[src]
+                nc.vector.tensor_tensor(
+                    out=levels[dst][:, first // 2 : first // 2 + count, :],
+                    in0=values[:, first : first + count, :],
+                    in1=values[:, first + count : first + 2 * count, :],
+                    op=op,
+                )
+
+        def times_sign(values):
+            nc.vector.tensor_tensor(out=values, in0=values, in1=sign_rows, op=ALU.mult)
+
         widen_x(0)
         turn_xh(0)
         group_xh()
+        extremes(None, 0, 2, 0)
+        extremes(None, 0, 2, 4)
         quantize_xh(0)
+        extremes(None, 0, 2, 8)
+        extremes(None, 0, 2, 12)
         prepare_biases()
         attn_lin(0)
         turn_bf16(sign_rows, sign_t)
@@ -374,12 +395,14 @@ def tile_decoderlstm_pa_t_w4_kernel(
         turn_xh(1)
         group_xh()
         widen_x(2)
-        apply_sign(0, 0)
-        apply_sign(0, 1)
-        max_level(0)
-        quantize_xh(1)
         for n in range(1, 4):
-            max_level(n)
+            extremes(n - 1, n, S >> (n + 1))
+        add_gate_biases()
+        times_sign(top[:])
+        times_sign(low_level[3][:, 0, :])
+        nc.vector.tensor_tensor(out=top[:], in0=top[:], in1=low_level[3][:, 0, :], op=ALU.max)
+        quantize_xh(1)
+        times_sign(top[:])
 
         last = TILES - 1
 
@@ -466,19 +489,16 @@ def tile_decoderlstm_pa_t_w4_kernel(
                 turn_c(i - 2, bank_b)
             if i + 3 <= last:
                 widen_x(i + 3)
-            fillers = []
+            max_level(0)
             if i + 2 <= last:
-                fillers.append(lambda: quantize_xh(i + 2))
+                quantize_xh(i + 2)
+            max_level(1)
             if i >= 2:
-                fillers.append(write_term)
+                write_term()
+            max_level(2)
             if i >= 1:
-                fillers.append(quantize_att)
-            for n in range(4):
-                if n == 3 and fillers:
-                    fillers.pop()()
-                max_level(n)
-                if n < 2 and len(fillers) > 1:
-                    fillers.pop(0)()
+                quantize_att()
+            max_level(3)
 
         held = ((GATE_F, bank_a), (GATE_I, sign_bank), (GATE_G, top_bank), (GATE_O, abs_bank))
         spread_top(0)
@@ -497,7 +517,6 @@ def tile_decoderlstm_pa_t_w4_kernel(
         sum_num(0)
         gate_sums(last - 2, GATE_F, sign_bank)
         gate_sums(last - 2, GATE_O, bank_a)
-        sum_num(1)
         score(last, 0)
         exp(last, 0)
         score(last, 1)
@@ -505,67 +524,70 @@ def tile_decoderlstm_pa_t_w4_kernel(
         diff(nc.vector, top_bank, last, 2)
         diff(nc.vector, top_bank, last, 3, GPSIMD_DIFF, S)
         weigh(nc.gpsimd, last, 0, 1)
+        sum_num(1)
         sum_num(2)
-        cell(last - 3)
         gate_tanh(GATE_F, sign_bank)
-        gate_tanh(GATE_O, bank_a)
         gate_sums_without_att(last - 1, *held[2])
         sum_num(3)
         score(last, 2)
         exp(last, 2)
         score(last, 3)
+        cell(last - 3)
         exp(last, 3)
+        gate_tanh(GATE_O, bank_a)
         weigh(nc.vector, last, 1, 1)
-        hidden(last - 3)
         normalise()
+        hidden(last - 3)
         gate_sums_without_att(last - 1, *held[1])
-        sum_den(last, 0)
-        att_to_rows(bank_c)
-        gate_sums_without_att(last - 1, *held[0])
-        turn_c(last - 2, bank_b)
-        sum_den(last, 1)
-        att_to_groups(bank_c)
-        gate_sums_without_att(last - 1, *held[3])
         sum_den(last, 2)
-        fold(prod_of(0, 2), HALF)
-        weigh(nc.vector, last, 2, 1)
+        att_to_rows(bank_c)
+        turn_c(last - 2, bank_b)
+        gate_sums_without_att(last - 1, *held[0])
+        fold(work_of(last, 0, 2), HALF)
+        att_to_groups(bank_c)
+        sum_den(last, 3)
+        gate_sums_without_att(last - 1, *held[3])
+        sum_den(last, 0, HALF)
+        sum_den(last, 1, HALF)
+        invert_den()
         write_term()
         keep_term(bank_b)
         quantize_att()
-        weigh(nc.vector, last, 3, 1)
-        fold(prod_of(2, 2), HALF)
-        sum_den(last, 3)
-        invert_den()
-        for g, dst in held:
-            gate_sums_of_att(g, dst)
+        fold(prod_of(0, 2), HALF)
+        weigh(nc.vector, last, 2, 1)
+        fold(prod_of(2), HALF)
+        weigh(nc.vector, last, 3, 1, slice(0, HALF))
+        weigh(nc.vector, last, 3, 1, slice(HALF, S))
         sum_num(0, HALF)
         sum_num(1, HALF)
-        cell(last - 2)
-        hidden(last - 2)
+        for g, dst in held:
+            gate_sums_of_att(g, dst)
+        sum_num(2, HALF)
+        sum_num(3)
+        normalise()
         for g, dst in held[:3]:
             gate_tanh(g, dst)
-        sum_num(2, HALF)
-        sum_num(3, HALF)
-        normalise()
         gate_sums_without_att(last, *held[0])
         att_to_rows(bank_c)
+        cell(last - 2, den_bank, num_bank)
+        hidden(last - 2, num_bank)
+        gate_tanh(*held[3])
+        att_to_groups(bank_c)
+        quantize_att()
         turn_c(last - 1, bank_b)
         write_term()
         keep_term(bank_b)
-        gate_tanh(*held[3])
-        gate_sums_without_att(last, *held[1])
-        att_to_groups(bank_c)
-        quantize_att()
-        gate_sums_without_att(last, *held[2])
-        gate_sums_without_att(last, *held[3])
-        cell(last - 1)
+        for g, dst in held[1:]:
+            gate_sums_without_att(last, g, dst)
         for g, dst in held:
             gate_sums_of_att(g, dst)
-        hidden(last - 1)
         turn_c(last, bank_b)
-        for g, dst in held:
+        for g, dst in held[:3]:
             gate_tanh(g, dst)
+        cell(last - 1, den_bank, num_bank)
         keep_term(bank_b)
         write_term()
+        gate_tanh(*held[3])
+        hidden(last - 1, num_bank)
         cell(last)
         hidden(last)

@@ -20,7 +20,7 @@ FP4X4 = mybir.dt.float4_e2m1fn_x4
 ACT = mybir.ActivationFunctionType
 ALU = mybir.AluOpType
 
-GPSIMD_DIFF = 11
+GPSIMD_DIFF = 9
 HALF = S // 2
 GATE_I, GATE_F, GATE_G, GATE_O = 0, 1, 2, 3
 
@@ -47,7 +47,9 @@ def tile_decoderlstm_pa_t_w4_kernel(
 
         ident32 = sbuf("ident32", [P, P], F32)
         ident16 = sbuf("ident16", [P, P], BF16)
-        ones = sbuf("ones", [P, H], BF16)
+        ones = sbuf("ones", [P, P], F32)
+        minus_ident16 = sbuf("minus_ident16", [P, P], BF16)
+        abs_rows = sbuf("abs_rows", [P, P], F32)
         bias_rows = sbuf("bias_rows", [P, P], BF16)
         bias_cols = sbuf("bias_cols", [P, 36], F32)
         gate_bias = sbuf("gate_bias", [P, 16], F32)
@@ -131,6 +133,9 @@ def tile_decoderlstm_pa_t_w4_kernel(
         make_identity(nc, ident32[:])
         make_identity(nc, ident16[:])
         nc.gpsimd.memset(ones[:], 1.0)
+        nc.gpsimd.tensor_scalar(
+            out=minus_ident16[:], in0=ident16[:], scalar1=-1.0, scalar2=0.0, op0=ALU.mult, op1=ALU.add
+        )
         nc.gpsimd.memset(wih_scales[:].bitcast(I32), 0)
         nc.gpsimd.memset(whh_scales[:].bitcast(I32), 0)
 
@@ -153,8 +158,8 @@ def tile_decoderlstm_pa_t_w4_kernel(
         nc.sync.dma_start(out=c_all[:], in_=c_prev.rearrange("(i p) k -> p i k", p=P))
 
         def prepare_biases():
-            nc.tensor.transpose(as_bf16(bank_c)[:, 0:P], bias_rows[:], ident16[:])
-            nc.scalar.copy(out=bias_cols[:], in_=as_bf16(bank_c)[:, 0:36])
+            nc.tensor.transpose(as_bf16(bank_a)[:, 0:P], bias_rows[:], ident16[:])
+            nc.scalar.copy(out=bias_cols[:], in_=as_bf16(bank_a)[:, 0:36])
 
         def add_gate_biases():
             nc.vector.tensor_tensor(out=gate_bias[:], in0=bias_cols[:, 0:16], in1=bias_cols[:, 16:32], op=ALU.add)
@@ -175,11 +180,11 @@ def tile_decoderlstm_pa_t_w4_kernel(
             nc.scalar.copy(out=x_wide[:], in_=src.bitcast(FP8))
 
         def turn_xh(i):
-            turn_words(bank_a, 0, x_wide[:])
-            turn_words(bank_a, 2 * P, h_first[:] if i == 0 else h_rest[:, i - 1, :])
+            turn_words(bank_b, 0, x_wide[:])
+            turn_words(bank_b, 2 * P, h_first[:] if i == 0 else h_rest[:, i - 1, :])
 
         def scale_x():
-            turned = as_bf16(bank_a).rearrange("p (u r e) -> p u e r", u=2, e=2)
+            turned = as_bf16(bank_b).rearrange("p (u r e) -> p u e r", u=2, e=2)
             for t in range(4):
                 nc.scalar.activation(
                     out=x_planes[:, t, :], in_=turned[:, t // 2, t % 2, :], func=ACT.Copy, scale=xs[:, t : t + 1]
@@ -189,7 +194,7 @@ def tile_decoderlstm_pa_t_w4_kernel(
             )
 
         def group_h():
-            group_words(xh_grouped[:, H:], bank_a[:, 2 * P :])
+            group_words(xh_grouped[:, H:], bank_b[:, 2 * P :])
 
         def quantize_xh(i):
             nc.vector.quantize_mx(out=xh_codes[i][:].bitcast(FP8X4), scales=xh_scales[i][:], in_=xh_grouped[:])
@@ -207,19 +212,19 @@ def tile_decoderlstm_pa_t_w4_kernel(
 
         def attn_lin(i):
             for c in range(CHUNKS):
-                mx(bank_a[:, cols(c)], wa_words, wa_scales, c, xh_codes[i][:, 0:P], xh_scales[i][:, 0:P], True, True)
+                mx(bank_c[:, cols(c)], wa_words, wa_scales, c, xh_codes[i][:, 0:P], xh_scales[i][:, 0:P], True, True)
             for c in range(CHUNKS):
                 nc.scalar.activation(
-                    out=sign_t[:, cols(c)], in_=bank_a[:, cols(c)], func=ACT.Sign, bias=bias_cols[:, 32 + c : 33 + c]
+                    out=sign_t[:, cols(c)], in_=bank_c[:, cols(c)], func=ACT.Sign, bias=bias_cols[:, 32 + c : 33 + c]
                 )
             for c in range(CHUNKS):
                 nc.scalar.activation(
-                    out=abs_t[:, cols(c)], in_=bank_a[:, cols(c)], func=ACT.Identity if i == 0 else ACT.Abs, bias=bias_cols[:, 32 + c : 33 + c]
+                    out=abs_t[:, cols(c)], in_=bank_c[:, cols(c)], func=ACT.Identity if i == 0 else ACT.Abs, bias=bias_cols[:, 32 + c : 33 + c]
                 )
 
         def turn_bf16(dst, src):
             for c in range(CHUNKS):
-                nc.tensor.matmul(dst[:, cols(c)], lhsT=src[:, cols(c)], rhs=ident16[:], start=True, stop=True)
+                nc.tensor.transpose(dst[:, cols(c)], src[:, cols(c)], ident16[:])
 
         def turn_abs():
             for c in range(CHUNKS):
@@ -249,17 +254,33 @@ def tile_decoderlstm_pa_t_w4_kernel(
                     out=level[n][:, :, js], in0=src[:, 0:count, js], in1=src[:, count:, js], op=ALU.max
                 )
 
+        def source_of(i):
+            return enc[0] if i == 0 else signed
+
         def diff(engine, largest, i, c, first=0, last=S):
             engine.tensor_tensor(
                 out=work_of(i, c)[:, first:last, :],
-                in0=(enc[0] if i == 0 else signed)[:, first:last, cols(c)],
+                in0=source_of(i)[:, first:last, cols(c)],
                 in1=over_s(largest[:, cols(c)], last - first),
                 op=ALU.subtract,
             )
 
-        def score(i, c):
-            w = work_of(i, c)
-            nc.vector.tensor_tensor(out=w, in0=w, in1=over_s(abs_bank[:, cols(c)]), op=ALU.mult)
+        def score(i, c, count=S):
+            w = work_of(i, c)[:, 0:count, :]
+            nc.vector.tensor_tensor(out=w, in0=w, in1=over_s(abs_bank[:, cols(c)], count), op=ALU.mult)
+
+        def diff_on_tensor(i, dst, first):
+            values = source_of(i)[:, first : first + 4, cols(2)]
+            nc.tensor.matmul(dst[:], lhsT=ident16[:], rhs=values, start=True, stop=False)
+            nc.tensor.matmul(dst[:], lhsT=minus_ident16[:], rhs=over_s(top[:, cols(2)], 4), start=False, stop=True)
+
+        def score_from_tensor(i, src, first):
+            nc.vector.tensor_tensor(
+                out=work_of(i, 2)[:, first : first + 4, :],
+                in0=src[:].rearrange("p (s j) -> p s j", j=P),
+                in1=over_s(abs_rows[:], 4),
+                op=ALU.mult,
+            )
 
         def exp(i, c):
             w = work_of(i, c)
@@ -326,12 +347,8 @@ def tile_decoderlstm_pa_t_w4_kernel(
             nc.scalar.activation(out=tanh_c[:], in_=c_bank[:], func=ACT.Tanh, scale=0.5)
             nc.scalar.activation(out=c_out[i % 2][:], in_=c_bank[:], func=ACT.Copy, scale=0.5)
             nc.sync.dma_start(out=out_1[rows(i), :], in_=c_out[i % 2][:])
-            nc.tensor.matmul(o_bank[:], lhsT=ident16[:], rhs=ones[:], start=True, stop=False)
             for c in range(CHUNKS):
-                nc.tensor.matmul(
-                    o_bank[:, cols(c)], lhsT=gate_t[GATE_O][:, cols(c)], rhs=ident32[:], start=False,
-                    stop=c == CHUNKS - 1, is_transpose=True,
-                )
+                turn_and_add(o_bank[:, cols(c)], [gate_t[GATE_O][:, cols(c)], ones[:]])
 
         def hidden(i, o_bank=bank_c):
             nc.vector.scalar_tensor_tensor(
@@ -416,15 +433,21 @@ def tile_decoderlstm_pa_t_w4_kernel(
                 diff(nc.gpsimd, top, i, 1)
             on_gpsimd = S if i == 0 else GPSIMD_DIFF
             diff(nc.gpsimd, top, i, 3, 0, on_gpsimd)
+            nc.scalar.copy(out=abs_rows[:], in_=abs_bank[:, cols(2)])
             if i >= 3:
                 keep_term(bank_b)
             diff(nc.vector, top_bank, i, 0)
-            attn_lin(i + 1)
+            if i == 0:
+                attn_lin(1)
             if i >= 2:
                 gate_sums(i - 2, GATE_I, sign_bank)
                 gate_tanh(GATE_I, sign_bank)
             if i >= 3:
                 cell(i - 3)
+            if i >= 2:
+                gate_sums(i - 2, GATE_G, bank_a)
+            if i >= 2:
+                gate_tanh(GATE_G, bank_a)
             if i + 2 <= last:
                 turn_xh(i + 2)
                 group_xh()
@@ -434,9 +457,9 @@ def tile_decoderlstm_pa_t_w4_kernel(
                 sum_num(0)
             if i + 2 <= last:
                 load_enc(i + 2)
-            if i >= 2:
-                gate_sums(i - 2, GATE_G, bank_b)
             spread_top(1)
+            diff_on_tensor(i, sign_bank, HALF)
+            diff_on_tensor(i, bank_a, HALF + 4)
             if i >= 1:
                 sum_num(1)
                 sum_den(i - 1, 2)
@@ -445,14 +468,14 @@ def tile_decoderlstm_pa_t_w4_kernel(
             exp(i, 0)
             score(i, 1)
             exp(i, 1)
+            score_from_tensor(i, sign_bank, HALF)
+            score_from_tensor(i, bank_a, HALF + 4)
             if i >= 3:
                 hidden(i - 3)
-            if i >= 2:
-                gate_tanh(GATE_G, bank_b)
             if i >= 1:
                 invert_den()
             turn_bf16(sign_rows, sign_t)
-            diff(nc.vector, top_bank, i, 2)
+            diff(nc.vector, top_bank, i, 2, 0, HALF)
             if i >= 1:
                 diff(nc.vector, top_bank, i, 3, on_gpsimd, S)
             if i == 0:
@@ -462,16 +485,16 @@ def tile_decoderlstm_pa_t_w4_kernel(
                 weigh(nc.gpsimd, i, 0, 2)
             if i >= 2:
                 gate_sums(i - 2, GATE_F, bank_a)
-            score(i, 2)
+                gate_sums(i - 2, GATE_O, bank_b)
+            score(i, 2, HALF)
             exp(i, 2)
             if i >= 2:
                 gate_tanh(GATE_F, bank_a)
+                gate_tanh(GATE_O, bank_b)
             score(i, 3)
             if i >= 1:
                 sum_num(2)
                 sum_num(3)
-            if i >= 2:
-                gate_sums(i - 2, GATE_O, bank_b)
             exp(i, 3)
             sum_den(i, 0)
             apply_sign(i + 1, 0)
@@ -480,8 +503,6 @@ def tile_decoderlstm_pa_t_w4_kernel(
             if i >= 1:
                 normalise()
                 att_to_rows(bank_c)
-            if i >= 2:
-                gate_tanh(GATE_O, bank_b)
             sum_den(i, 1)
             if i >= 1:
                 att_to_groups(bank_a)
@@ -492,6 +513,7 @@ def tile_decoderlstm_pa_t_w4_kernel(
             max_level(0)
             if i + 2 <= last:
                 quantize_xh(i + 2)
+                attn_lin(i + 2)
             max_level(1)
             if i >= 2:
                 write_term()
@@ -503,6 +525,7 @@ def tile_decoderlstm_pa_t_w4_kernel(
         held = ((GATE_F, bank_a), (GATE_I, sign_bank), (GATE_G, top_bank), (GATE_O, abs_bank))
         spread_top(0)
         diff(nc.gpsimd, top, last, 3, 0, GPSIMD_DIFF)
+        nc.scalar.copy(out=abs_rows[:], in_=abs_bank[:, cols(2)])
         keep_term(bank_b)
         diff(nc.vector, top_bank, last, 0)
         for g, dst in ((GATE_I, sign_bank), (GATE_G, bank_a)):
@@ -514,22 +537,26 @@ def tile_decoderlstm_pa_t_w4_kernel(
         diff(nc.vector, top_bank, last, 1)
         weigh(nc.gpsimd, last - 1, 2, 2)
         spread_top(1)
+        diff_on_tensor(last, sign_bank, HALF)
+        diff_on_tensor(last, bank_a, HALF + 4)
         sum_num(0)
-        gate_sums(last - 2, GATE_F, sign_bank)
-        gate_sums(last - 2, GATE_O, bank_a)
+        sum_num(1)
         score(last, 0)
         exp(last, 0)
         score(last, 1)
         exp(last, 1)
-        diff(nc.vector, top_bank, last, 2)
+        score_from_tensor(last, sign_bank, HALF)
+        score_from_tensor(last, bank_a, HALF + 4)
+        gate_sums(last - 2, GATE_F, sign_bank)
+        gate_sums(last - 2, GATE_O, bank_a)
+        diff(nc.vector, top_bank, last, 2, 0, HALF)
         diff(nc.vector, top_bank, last, 3, GPSIMD_DIFF, S)
         weigh(nc.gpsimd, last, 0, 1)
-        sum_num(1)
         sum_num(2)
         gate_tanh(GATE_F, sign_bank)
         gate_sums_without_att(last - 1, *held[2])
         sum_num(3)
-        score(last, 2)
+        score(last, 2, HALF)
         exp(last, 2)
         score(last, 3)
         cell(last - 3)
@@ -562,22 +589,22 @@ def tile_decoderlstm_pa_t_w4_kernel(
         sum_num(1, HALF)
         for g, dst in held:
             gate_sums_of_att(g, dst)
+        cell(last - 2)
+        for g, dst in held:
+            gate_tanh(g, dst)
         sum_num(2, HALF)
         sum_num(3)
         normalise()
-        for g, dst in held[:3]:
-            gate_tanh(g, dst)
+        hidden(last - 2)
         gate_sums_without_att(last, *held[0])
         att_to_rows(bank_c)
-        cell(last - 2, den_bank, num_bank)
-        hidden(last - 2, num_bank)
-        gate_tanh(*held[3])
-        att_to_groups(bank_c)
-        quantize_att()
         turn_c(last - 1, bank_b)
         write_term()
         keep_term(bank_b)
-        for g, dst in held[1:]:
+        gate_sums_without_att(last, *held[1])
+        att_to_groups(bank_c)
+        quantize_att()
+        for g, dst in held[2:]:
             gate_sums_without_att(last, g, dst)
         for g, dst in held:
             gate_sums_of_att(g, dst)

from contextlib import ExitStack

import concourse.mybir as mybir
from concourse.masks import make_identity

B, H, S = 1024, 512, 16
P = 128
TILES = B // P
CHUNKS = H // P
FLOPS = 2 * B * H * (H + 3 * 4 * H)

F32 = mybir.dt.float32
BF16 = mybir.dt.bfloat16
I32 = mybir.dt.int32
U32 = mybir.dt.uint32
U8 = mybir.dt.uint8
FP8 = mybir.dt.float8_e4m3fn
FP8X4 = mybir.dt.float8_e4m3fn_x4
FP4X4 = mybir.dt.float4_e2m1fn_x4
ACT = mybir.ActivationFunctionType
ALU = mybir.AluOpType

GPSIMD_DIFF = 9
HALF = S // 2
GATE_I, GATE_F, GATE_G, GATE_O = 0, 1, 2, 3


def tile_decoderlstm_pa_t_w4_kernel(
    tc, x_bytes, x_scale, enc_seq, attn_W_words, attn_W_scales, attn_b, h_prev, c_prev,
    W_ih0_words, W_ih0_scales, W_hh0_words, W_hh0_scales, b_ih0, b_hh0, out_0, out_1,
):
    nc = tc.nc
    with ExitStack() as ctx:
        sb = ctx.enter_context(tc.tile_pool(name="sb", bufs=1))
        ps = ctx.enter_context(tc.psum_pool(name="ps", bufs=1))
        ctx.enter_context(tc.manual_schedule())

        def sbuf(name, shape, dtype):
            return sb.tile(shape, dtype, name=name, align_bytes=64)

        def bank(name):
            return ps.tile([P, H], F32, name=name)

        abs_bank, sign_bank, top_bank = bank("abs_bank"), bank("sign_bank"), bank("top_bank")
        den_bank, num_bank = bank("den_bank"), bank("num_bank")
        bank_a, bank_b, bank_c = bank("bank_a"), bank("bank_b"), bank("bank_c")

        ident32 = sbuf("ident32", [P, P], F32)
        ident16 = sbuf("ident16", [P, P], BF16)
        ones = sbuf("ones", [P, P], F32)
        minus_ident16 = sbuf("minus_ident16", [P, P], BF16)
        abs_rows = sbuf("abs_rows", [P, P], F32)
        bias_rows = sbuf("bias_rows", [P, P], BF16)
        bias_cols = sbuf("bias_cols", [P, 36], F32)
        gate_bias = sbuf("gate_bias", [P, 16], F32)
        half_gate_bias = sbuf("half_gate_bias", [P, 16], F32)
        xs = sbuf("xs", [P, 4], F32)
        xb_first = sbuf("xb_first", [P, H], U8)
        xb_rest = sbuf("xb_rest", [P, TILES - 1, H], U8)
        h_first = sbuf("h_first", [P, H], BF16)
        h_rest = sbuf("h_rest", [P, TILES - 1, H], BF16)
        c_all = sbuf("c_all", [P, TILES, H], BF16)
        wa_words = sbuf("wa_words", [P, 2 * H], U8)
        wa_scales = sbuf("wa_scales", [P, H], U8)
        wih_words = sbuf("wih_words", [P, 2, 8 * H], U8)
        wih_scales = sbuf("wih_scales", [P, 2, 4 * H], U8)
        whh_words = sbuf("whh_words", [P, 8 * H], U8)
        whh_scales = sbuf("whh_scales", [P, 4 * H], U8)

        enc = [sbuf("enc%d" % n, [P, S, H], BF16) for n in range(3)]
        signed = sbuf("signed", [P, S, H], BF16)
        top = sbuf("top", [P, H], BF16)
        early_work = sbuf("early_work", [P, S, 2 * P], F32)
        late_work = [sbuf("late_work%d" % n, [P, S, 2 * P], F32) for n in range(2)]
        prod = [sbuf("prod%d" % n, [P, S, 2 * P], F32) for n in range(2)]
        scratch = prod[1][:].rearrange("p s j -> p (s j)").bitcast(BF16).rearrange("p (s j) -> p s j", j=H)
        level = [scratch[:, 0:8, :], scratch[:, 8:12, :], scratch[:, 12:14, :], top[:].unsqueeze(1)]
        spare = prod[0][:].rearrange("p s j -> p (s j)").bitcast(BF16).rearrange("p (s j) -> p s j", j=H)
        low_level = [spare[:, 0:8, :], spare[:, 8:12, :], spare[:, 12:14, :], spare[:, 14:15, :]]

        x_wide = sbuf("x_wide", [P, H], BF16)
        x_planes = sbuf("x_planes", [P, 4, P], BF16)
        xh_grouped = sbuf("xh_grouped", [P, 2 * H], BF16)
        xh_codes = [sbuf("xh_codes%d" % n, [P, 2 * P], U32) for n in range(TILES)]
        xh_scales = [sbuf("xh_scales%d" % n, [P, 2 * P], U8) for n in range(TILES)]
        abs_t = sbuf("abs_t", [P, H], F32)
        sign_t = sbuf("sign_t", [P, H], BF16)
        inv_den = sbuf("inv_den", [P, H], F32)
        att_t = sbuf("att_t", [P, H], BF16)
        att_rows = sbuf("att_rows", [P, H], BF16)
        att_grouped = sbuf("att_grouped", [P, H], BF16)
        att_codes = sbuf("att_codes", [P, P], U32)
        att_scales = sbuf("att_scales", [P, P], U8)
        gate_t = [sbuf("gate_t%d" % n, [P, H], F32) for n in range(4)]
        keep_t = sbuf("keep_t", [P, H], F32)
        write_t = sbuf("write_t", [P, H], F32)
        tanh_c = sbuf("tanh_c", [P, H], F32)
        c_out = [sbuf("c_out%d" % n, [P, H], F32) for n in range(2)]
        h_out = [sbuf("h_out%d" % n, [P, H], F32) for n in range(2)]

        def cols(c):
            return slice(c * P, (c + 1) * P)

        def rows(i):
            return slice(i * P, (i + 1) * P)

        def over_s(ap, count=S):
            return ap.unsqueeze(1).to_broadcast([P, count, P])

        def as_bf16(psum_tile):
            return psum_tile[:].bitcast(BF16)[:, 0:H]

        sign_rows = as_bf16(sign_bank)

        def work_of(i, first, count=1):
            pair = early_work if first < 2 else late_work[i % 2]
            return pair[:, :, (first % 2) * P : (first % 2 + count) * P]

        def prod_of(first, count=1):
            return prod[first // 2][:, :, (first % 2) * P : (first % 2 + count) * P]

        def load_scales(plane, scales):
            for q in range(4):
                nc.sync.dma_start(out=plane[32 * q : 32 * q + 4].bitcast(I32), in_=scales(slice(4 * q, 4 * q + 4)))

        def load_enc(i, parts=2):
            for part in range(parts):
                ss = slice(part * S // parts, (part + 1) * S // parts)
                nc.sync.dma_start(out=enc[i % 3][:, ss, :], in_=enc_seq[ss, rows(i), :].rearrange("s b j -> b s j"))

        nc.gpsimd.memset(wa_scales[:].bitcast(I32), 0)
        nc.gpsimd.memset(bias_rows[:], 0.0)
        make_identity(nc, ident32[:])
        make_identity(nc, ident16[:])
        nc.gpsimd.memset(ones[:], 1.0)
        nc.gpsimd.tensor_scalar(
            out=minus_ident16[:], in0=ident16[:], scalar1=-1.0, scalar2=0.0, op0=ALU.mult, op1=ALU.add
        )
        nc.gpsimd.memset(wih_scales[:].bitcast(I32), 0)
        nc.gpsimd.memset(whh_scales[:].bitcast(I32), 0)

        nc.sync.dma_start(out=xb_first[:], in_=x_bytes[rows(0), :])
        nc.sync.dma_start(out=h_first[:], in_=h_prev[rows(0), :])
        nc.sync.dma_start(out=xs[:], in_=x_scale.rearrange("o (p t) -> p (o t)", t=4))
        nc.sync.dma_start(out=wa_words[:].bitcast(I32), in_=attn_W_words[0].bitcast(I32))
        load_enc(0, 4)
        load_scales(wa_scales, lambda r: attn_W_scales[0, r, :].bitcast(I32))
        nc.sync.dma_start(out=bias_rows[32:36, :], in_=attn_b.rearrange("(c m) -> c m", m=P))
        nc.sync.dma_start(out=bias_rows[0:16, :], in_=b_ih0.rearrange("(c m) -> c m", m=P))
        nc.sync.dma_start(out=bias_rows[16:32, :], in_=b_hh0.rearrange("(c m) -> c m", m=P))
        nc.sync.dma_start(out=xb_rest[:], in_=x_bytes[P:, :].rearrange("(i p) k -> p i k", p=P))
        nc.sync.dma_start(out=h_rest[:], in_=h_prev[P:, :].rearrange("(i p) k -> p i k", p=P))
        load_enc(1)
        nc.sync.dma_start(out=wih_words[:].bitcast(I32), in_=W_ih0_words.bitcast(I32).rearrange("g p n -> p g n"))
        nc.sync.dma_start(out=whh_words[:].bitcast(I32), in_=W_hh0_words[0].bitcast(I32))
        load_scales(wih_scales, lambda r: W_ih0_scales[:, r, :].bitcast(I32).rearrange("g r n -> r g n"))
        load_scales(whh_scales, lambda r: W_hh0_scales[0, r, :].bitcast(I32))
        nc.sync.dma_start(out=c_all[:], in_=c_prev.rearrange("(i p) k -> p i k", p=P))

        def prepare_biases():
            nc.tensor.transpose(as_bf16(bank_a)[:, 0:P], bias_rows[:], ident16[:])
            nc.scalar.copy(out=bias_cols[:], in_=as_bf16(bank_a)[:, 0:36])

        def add_gate_biases():
            nc.vector.tensor_tensor(out=gate_bias[:], in0=bias_cols[:, 0:16], in1=bias_cols[:, 16:32], op=ALU.add)
            nc.vector.tensor_scalar(out=half_gate_bias[:], in0=gate_bias[:], scalar1=0.5, scalar2=None, op0=ALU.mult)

        def turn_words(dst, first_col, src):
            words = src.bitcast(F32)
            for u in range(2):
                nc.tensor.transpose(dst[:, first_col + u * P : first_col + (u + 1) * P], words[:, u::2], ident32[:])

        def group_words(dst, src):
            nc.scalar.copy(
                out=dst.bitcast(F32).rearrange("p (r u) -> p r u", u=2), in_=src.rearrange("p (u r) -> p r u", u=2)
            )

        def widen_x(i):
            src = xb_first[:] if i == 0 else xb_rest[:, i - 1, :]
            nc.scalar.copy(out=x_wide[:], in_=src.bitcast(FP8))

        def turn_xh(i):
            turn_words(bank_b, 0, x_wide[:])
            turn_words(bank_b, 2 * P, h_first[:] if i == 0 else h_rest[:, i - 1, :])

        def scale_x():
            turned = as_bf16(bank_b).rearrange("p (u r e) -> p u e r", u=2, e=2)
            for t in range(4):
                nc.scalar.activation(
                    out=x_planes[:, t, :], in_=turned[:, t // 2, t % 2, :], func=ACT.Copy, scale=xs[:, t : t + 1]
                )
            nc.scalar.copy(
                out=xh_grouped[:, 0:H].rearrange("p (r t) -> p r t", t=4), in_=x_planes[:].rearrange("p t r -> p r t")
            )

        def group_h():
            group_words(xh_grouped[:, H:], bank_b[:, 2 * P :])

        def quantize_xh(i):
            nc.vector.quantize_mx(out=xh_codes[i][:].bitcast(FP8X4), scales=xh_scales[i][:], in_=xh_grouped[:])

        def mx(dst, words, scales, n, codes, code_scales, start, stop):
            nc.tensor.matmul_mx(
                out=dst,
                lhsT=words[:, 2 * P * n : 2 * P * (n + 1)].bitcast(FP4X4),
                lhsT_scale=scales[:, cols(n)],
                rhs=codes.bitcast(FP8X4),
                rhs_scale=code_scales,
                start=start,
                stop=stop,
            )

        def attn_lin(i):
            for c in range(CHUNKS):
                mx(bank_c[:, cols(c)], wa_words, wa_scales, c, xh_codes[i][:, 0:P], xh_scales[i][:, 0:P], True, True)
            for c in range(CHUNKS):
                nc.scalar.activation(
                    out=sign_t[:, cols(c)], in_=bank_c[:, cols(c)], func=ACT.Sign, bias=bias_cols[:, 32 + c : 33 + c]
                )
            for c in range(CHUNKS):
                nc.scalar.activation(
                    out=abs_t[:, cols(c)], in_=bank_c[:, cols(c)], func=ACT.Identity if i == 0 else ACT.Abs, bias=bias_cols[:, 32 + c : 33 + c]
                )

        def turn_bf16(dst, src):
            for c in range(CHUNKS):
                nc.tensor.transpose(dst[:, cols(c)], src[:, cols(c)], ident16[:])

        def turn_abs():
            for c in range(CHUNKS):
                nc.tensor.transpose(abs_bank[:, cols(c)], abs_t[:, cols(c)], ident32[:])

        def turn_and_add(dst, terms):
            for n, term in enumerate(terms):
                nc.tensor.matmul(
                    dst, lhsT=term, rhs=ident32[:], start=n == 0, stop=n == len(terms) - 1, is_transpose=True
                )

        def apply_sign(i, half):
            ss = slice(half * S // 2, (half + 1) * S // 2)
            nc.vector.tensor_tensor(
                out=signed[:, ss, :],
                in0=enc[i % 3][:, ss, :],
                in1=sign_rows.unsqueeze(1).to_broadcast([P, S // 2, H]),
                op=ALU.mult,
            )

        def max_level(n):
            src = signed if n == 0 else level[n - 1]
            count = S >> (n + 1)
            for half in range(2):
                js = slice(half * H // 2, (half + 1) * H // 2)
                nc.vector.tensor_tensor(
                    out=level[n][:, :, js], in0=src[:, 0:count, js], in1=src[:, count:, js], op=ALU.max
                )

        def source_of(i):
            return enc[0] if i == 0 else signed

        def diff(engine, largest, i, c, first=0, last=S):
            engine.tensor_tensor(
                out=work_of(i, c)[:, first:last, :],
                in0=source_of(i)[:, first:last, cols(c)],
                in1=over_s(largest[:, cols(c)], last - first),
                op=ALU.subtract,
            )

        def score(i, c, count=S):
            w = work_of(i, c)[:, 0:count, :]
            nc.vector.tensor_tensor(out=w, in0=w, in1=over_s(abs_bank[:, cols(c)], count), op=ALU.mult)

        def diff_on_tensor(i, dst, first):
            values = source_of(i)[:, first : first + 4, cols(2)]
            nc.tensor.matmul(dst[:], lhsT=ident16[:], rhs=values, start=True, stop=False)
            nc.tensor.matmul(dst[:], lhsT=minus_ident16[:], rhs=over_s(top[:, cols(2)], 4), start=False, stop=True)

        def score_from_tensor(i, src, first):
            nc.vector.tensor_tensor(
                out=work_of(i, 2)[:, first : first + 4, :],
                in0=src[:].rearrange("p (s j) -> p s j", j=P),
                in1=over_s(abs_rows[:], 4),
                op=ALU.mult,
            )

        def exp(i, c):
            w = work_of(i, c)
            nc.scalar.activation(out=w, in_=w, func=ACT.Exp)

        def weigh(engine, i, first, count, ss=slice(0, S)):
            engine.tensor_tensor(
                out=prod_of(first, count)[:, ss, :],
                in0=work_of(i, first, count)[:, ss, :],
                in1=enc[i % 3][:, ss, first * P : (first + count) * P],
                op=ALU.mult,
            )

        def fold(terms, count):
            nc.vector.tensor_tensor(
                out=terms[:, 0:count, :], in0=terms[:, 0:count, :], in1=terms[:, count : 2 * count, :], op=ALU.add
            )

        def sum_den(i, c, count=S):
            turn_and_add(den_bank[:, cols(c)], [work_of(i, c)[:, s, :] for s in range(count)])

        def sum_num(c, count=S):
            turn_and_add(num_bank[:, cols(c)], [prod_of(c)[:, s, :] for s in range(count)])

        def invert_den():
            nc.scalar.activation(out=inv_den[:], in_=den_bank[:], func=ACT.Ln)
            nc.scalar.activation(out=inv_den[:], in_=inv_den[:], func=ACT.Exp, scale=-1.0)

        def gate_sums(i, g, dst):
            for c in range(CHUNKS):
                n = CHUNKS * g + c
                mx(dst[:, cols(c)], wih_words[:, 0, :], wih_scales[:, 0, :], n,
                   xh_codes[i][:, 0:P], xh_scales[i][:, 0:P], True, False)
                mx(dst[:, cols(c)], whh_words, whh_scales, n, xh_codes[i][:, P:], xh_scales[i][:, P:], False, False)
                mx(dst[:, cols(c)], wih_words[:, 1, :], wih_scales[:, 1, :], n,
                   att_codes[:], att_scales[:], False, True)

        def gate_sums_without_att(i, g, dst):
            for c in range(CHUNKS):
                n = CHUNKS * g + c
                mx(dst[:, cols(c)], wih_words[:, 0, :], wih_scales[:, 0, :], n,
                   xh_codes[i][:, 0:P], xh_scales[i][:, 0:P], c == 0, False)
                mx(dst[:, cols(c)], whh_words, whh_scales, n, xh_codes[i][:, P:], xh_scales[i][:, P:], False, False)

        def gate_sums_of_att(g, dst):
            for c in range(CHUNKS):
                mx(dst[:, cols(c)], wih_words[:, 1, :], wih_scales[:, 1, :], CHUNKS * g + c,
                   att_codes[:], att_scales[:], False, c == CHUNKS - 1)

        def gate_tanh(g, dst):
            bias, scale = (gate_bias, 1.0) if g == GATE_G else (half_gate_bias, 0.5)
            for c in range(CHUNKS):
                n = CHUNKS * g + c
                nc.scalar.activation(
                    out=gate_t[g][:, cols(c)], in_=dst[:, cols(c)], func=ACT.Tanh, bias=bias[:, n : n + 1], scale=scale
                )

        def one_plus_times(dst, a, b):
            nc.vector.scalar_tensor_tensor(out=dst, in0=a, scalar=1.0, in1=b, op0=ALU.add, op1=ALU.mult)

        def cell(i, c_bank=bank_b, o_bank=bank_c):
            for c in range(CHUNKS):
                turn_and_add(c_bank[:, cols(c)], [keep_t[:, cols(c)], write_t[:, cols(c)]])
            nc.scalar.activation(out=tanh_c[:], in_=c_bank[:], func=ACT.Tanh, scale=0.5)
            nc.scalar.activation(out=c_out[i % 2][:], in_=c_bank[:], func=ACT.Copy, scale=0.5)
            nc.sync.dma_start(out=out_1[rows(i), :], in_=c_out[i % 2][:])
            for c in range(CHUNKS):
                turn_and_add(o_bank[:, cols(c)], [gate_t[GATE_O][:, cols(c)], ones[:]])

        def hidden(i, o_bank=bank_c):
            nc.vector.scalar_tensor_tensor(
                out=h_out[i % 2][:], in0=o_bank[:], scalar=0.5, in1=tanh_c[:], op0=ALU.mult, op1=ALU.mult
            )
            nc.sync.dma_start(out=out_0[rows(i), :], in_=h_out[i % 2][:])

        def normalise():
            nc.vector.tensor_tensor(out=att_t[:], in0=num_bank[:], in1=inv_den[:], op=ALU.mult)

        def att_to_rows(dst):
            turn_bf16(as_bf16(dst), att_t)
            nc.scalar.copy(out=att_rows[:], in_=as_bf16(dst))

        def att_to_groups(dst):
            turn_words(dst, 0, att_rows[:])
            group_words(att_grouped[:], dst[:, 0 : 2 * P])

        def quantize_att():
            nc.vector.quantize_mx(out=att_codes[:].bitcast(FP8X4), scales=att_scales[:], in_=att_grouped[:])

        def keep_term(src):
            one_plus_times(keep_t[:], gate_t[GATE_F][:], as_bf16(src))

        def write_term():
            one_plus_times(write_t[:], gate_t[GATE_I][:], gate_t[GATE_G][:])

        def turn_c(i, dst):
            turn_bf16(as_bf16(dst), c_all[:, i, :])

        def group_xh():
            group_h()
            scale_x()

        def extremes(src, dst, count, first=0):
            for levels, op in ((level, ALU.max), (low_level, ALU.min)):
                values = enc[0] if src is None else levels[src]
                nc.vector.tensor_tensor(
                    out=levels[dst][:, first // 2 : first // 2 + count, :],
                    in0=values[:, first : first + count, :],
                    in1=values[:, first + count : first + 2 * count, :],
                    op=op,
                )

        def times_sign(values):
            nc.vector.tensor_tensor(out=values, in0=values, in1=sign_rows, op=ALU.mult)

        widen_x(0)
        turn_xh(0)
        group_xh()
        extremes(None, 0, 2, 0)
        extremes(None, 0, 2, 4)
        quantize_xh(0)
        extremes(None, 0, 2, 8)
        extremes(None, 0, 2, 12)
        prepare_biases()
        attn_lin(0)
        turn_bf16(sign_rows, sign_t)
        turn_abs()
        widen_x(1)
        turn_xh(1)
        group_xh()
        widen_x(2)
        for n in range(1, 4):
            extremes(n - 1, n, S >> (n + 1))
        add_gate_biases()
        times_sign(top[:])
        times_sign(low_level[3][:, 0, :])
        nc.vector.tensor_tensor(out=top[:], in0=top[:], in1=low_level[3][:, 0, :], op=ALU.max)
        quantize_xh(1)
        times_sign(top[:])

        last = TILES - 1

        def spread_top(half):
            js = slice(half * H // 2, (half + 1) * H // 2)
            nc.tensor.matmul(top_bank[:, js], lhsT=ident16[:], rhs=top[:, js], start=True, stop=True)

        for i in range(last):
            spread_top(0)
            if i == 0:
                diff(nc.gpsimd, top, i, 1)
            on_gpsimd = S if i == 0 else GPSIMD_DIFF
            diff(nc.gpsimd, top, i, 3, 0, on_gpsimd)
            nc.scalar.copy(out=abs_rows[:], in_=abs_bank[:, cols(2)])
            if i >= 3:
                keep_term(bank_b)
            diff(nc.vector, top_bank, i, 0)
            if i == 0:
                attn_lin(1)
            if i >= 2:
                gate_sums(i - 2, GATE_I, sign_bank)
                gate_tanh(GATE_I, sign_bank)
            if i >= 3:
                cell(i - 3)
            if i >= 2:
                gate_sums(i - 2, GATE_G, bank_a)
            if i >= 2:
                gate_tanh(GATE_G, bank_a)
            if i + 2 <= last:
                turn_xh(i + 2)
                group_xh()
            if i >= 1:
                diff(nc.vector, top_bank, i, 1)
                weigh(nc.gpsimd, i - 1, 2, 2)
                sum_num(0)
            if i + 2 <= last:
                load_enc(i + 2)
            spread_top(1)
            diff_on_tensor(i, sign_bank, HALF)
            diff_on_tensor(i, bank_a, HALF + 4)
            if i >= 1:
                sum_num(1)
                sum_den(i - 1, 2)
                sum_den(i - 1, 3)
            score(i, 0)
            exp(i, 0)
            score(i, 1)
            exp(i, 1)
            score_from_tensor(i, sign_bank, HALF)
            score_from_tensor(i, bank_a, HALF + 4)
            if i >= 3:
                hidden(i - 3)
            if i >= 1:
                invert_den()
            turn_bf16(sign_rows, sign_t)
            diff(nc.vector, top_bank, i, 2, 0, HALF)
            if i >= 1:
                diff(nc.vector, top_bank, i, 3, on_gpsimd, S)
            if i == 0:
                weigh(nc.gpsimd, i, 0, 1)
                weigh(nc.gpsimd, i, 1, 1)
            else:
                weigh(nc.gpsimd, i, 0, 2)
            if i >= 2:
                gate_sums(i - 2, GATE_F, bank_a)
                gate_sums(i - 2, GATE_O, bank_b)
            score(i, 2, HALF)
            exp(i, 2)
            if i >= 2:
                gate_tanh(GATE_F, bank_a)
                gate_tanh(GATE_O, bank_b)
            score(i, 3)
            if i >= 1:
                sum_num(2)
                sum_num(3)
            exp(i, 3)
            sum_den(i, 0)
            apply_sign(i + 1, 0)
            apply_sign(i + 1, 1)
            turn_abs()
            if i >= 1:
                normalise()
                att_to_rows(bank_c)
            sum_den(i, 1)
            if i >= 1:
                att_to_groups(bank_a)
            if i >= 2:
                turn_c(i - 2, bank_b)
            if i + 3 <= last:
                widen_x(i + 3)
            max_level(0)
            if i + 2 <= last:
                quantize_xh(i + 2)
                attn_lin(i + 2)
            max_level(1)
            if i >= 2:
                write_term()
            max_level(2)
            if i >= 1:
                quantize_att()
            max_level(3)

        held = ((GATE_F, bank_a), (GATE_I, sign_bank), (GATE_G, top_bank), (GATE_O, abs_bank))
        spread_top(0)
        diff(nc.gpsimd, top, last, 3, 0, GPSIMD_DIFF)
        nc.scalar.copy(out=abs_rows[:], in_=abs_bank[:, cols(2)])
        keep_term(bank_b)
        diff(nc.vector, top_bank, last, 0)
        for g, dst in ((GATE_I, sign_bank), (GATE_G, bank_a)):
            gate_sums(last - 2, g, dst)
            gate_tanh(g, dst)
        sum_den(last - 1, 2)
        sum_den(last - 1, 3)
        invert_den()
        diff(nc.vector, top_bank, last, 1)
        weigh(nc.gpsimd, last - 1, 2, 2)
        spread_top(1)
        diff_on_tensor(last, sign_bank, HALF)
        diff_on_tensor(last, bank_a, HALF + 4)
        sum_num(0)
        sum_num(1)
        score(last, 0)
        exp(last, 0)
        score(last, 1)
        exp(last, 1)
        score_from_tensor(last, sign_bank, HALF)
        score_from_tensor(last, bank_a, HALF + 4)
        gate_sums(last - 2, GATE_F, sign_bank)
        gate_sums(last - 2, GATE_O, bank_a)
        diff(nc.vector, top_bank, last, 2, 0, HALF)
        diff(nc.vector, top_bank, last, 3, GPSIMD_DIFF, S)
        weigh(nc.gpsimd, last, 0, 1)
        sum_num(2)
        gate_tanh(GATE_F, sign_bank)
        gate_sums_without_att(last - 1, *held[2])
        sum_num(3)
        score(last, 2, HALF)
        exp(last, 2)
        score(last, 3)
        cell(last - 3)
        exp(last, 3)
        gate_tanh(GATE_O, bank_a)
        weigh(nc.vector, last, 1, 1)
        normalise()
        hidden(last - 3)
        gate_sums_without_att(last - 1, *held[1])
        sum_den(last, 2)
        att_to_rows(bank_c)
        turn_c(last - 2, bank_b)
        gate_sums_without_att(last - 1, *held[0])
        fold(work_of(last, 0, 2), HALF)
        att_to_groups(bank_c)
        sum_den(last, 3)
        gate_sums_without_att(last - 1, *held[3])
        sum_den(last, 0, HALF)
        sum_den(last, 1, HALF)
        invert_den()
        write_term()
        keep_term(bank_b)
        quantize_att()
        fold(prod_of(0, 2), HALF)
        weigh(nc.vector, last, 2, 1)
        fold(prod_of(2), HALF)
        weigh(nc.vector, last, 3, 1, slice(0, HALF))
        weigh(nc.vector, last, 3, 1, slice(HALF, S))
        sum_num(0, HALF)
        sum_num(1, HALF)
        for g, dst in held:
            gate_sums_of_att(g, dst)
        cell(last - 2)
        for g, dst in held:
            gate_tanh(g, dst)
        sum_num(2, HALF)
        sum_num(3)
        normalise()
        hidden(last - 2)
        gate_sums_without_att(last, *held[0])
        att_to_rows(bank_c)
        turn_c(last - 1, bank_b)
        write_term()
        keep_term(bank_b)
        gate_sums_without_att(last, *held[1])
        att_to_groups(bank_c)
        quantize_att()
        for g, dst in held[2:]:
            gate_sums_without_att(last, g, dst)
        for g, dst in held:
            gate_sums_of_att(g, dst)
        turn_c(last, bank_b)
        for g, dst in held[:3]:
            gate_tanh(g, dst)
        cell(last - 1, den_bank, num_bank)
        keep_term(bank_b)
        write_term()
        gate_tanh(*held[3])
        hidden(last - 1, num_bank)
        cell(last)
        hidden(last)
